import numpy as np
import ml_dtypes


def mxq(x, axis, fmt="e4m3"):
    dtype, down = {"e4m3": (ml_dtypes.float8_e4m3fn, 7), "e5m2": (ml_dtypes.float8_e5m2, 14)}[fmt]
    v = np.moveaxis(np.asarray(x, np.float32).astype(ml_dtypes.bfloat16).astype(np.float64), axis, -1)
    blocks = v.reshape(v.shape[:-1] + (-1, 32))
    amax = np.abs(blocks).max(-1, keepdims=True)
    byte = np.maximum(np.where(amax > 0, np.frexp(amax)[1] - 1 + 127, 0) - down, 1)
    scale = np.exp2(byte - 127.0)
    codes = (blocks / scale).astype(np.float32).astype(dtype).astype(np.float64)
    return np.moveaxis((codes * scale).reshape(v.shape), -1, axis)


WIDE = False


def mx_kscale(k):
    if not WIDE:
        return np.ones(k)
    levels = np.array([10, -10, 5, -5, 0])
    a = np.random.permutation(np.resize(levels, k // 512 * 4)).reshape(k // 512, 4)
    idx = np.arange(k)
    return np.exp2(a[idx // 512, idx % 128 // 32])


BF16 = ml_dtypes.bfloat16


def bf(x):
    return np.asarray(x, np.float32).astype(BF16)


def f64(x):
    return np.asarray(x).astype(np.float64)


B, LQ, LK, D = 2, 512, 512, 512
EPS = 1e-8


def softmax(v):
    e = np.exp(v - v.max(-1, keepdims=True))
    return e / e.sum(-1, keepdims=True)


def setup_inputs():
    s = mx_kscale(D)
    sc = 1.0 / np.sqrt(D)
    base = np.array([0.0, 1.5, 0.5])
    return {
        "query": bf(np.random.standard_normal((B, LQ, D)) * s),
        "key": bf(np.random.standard_normal((B, LK, D)) * s),
        "Wq": bf(np.random.standard_normal((D, D)) * sc / s[None, :]),
        "bq": bf(np.random.standard_normal(D) * 0.2),
        "Wk": bf(np.random.standard_normal((D, D)) * sc / s[None, :]),
        "bk": bf(np.random.standard_normal(D) * 0.2),
        "scoring_weights": bf(base + 0.1 * np.random.standard_normal(base.shape)),
    }


def reference(query, key, Wq, bq, Wk, bk, scoring_weights):
    q = np.tanh((mxq(f64(query), 2, "e4m3") @ mxq(f64(Wq), 1, "e4m3").T) + f64(bq))
    k = np.tanh((mxq(f64(key), 2, "e4m3") @ mxq(f64(Wk), 1, "e4m3").T) + f64(bk))
    dot = mxq(q, 2, "e4m3") @ mxq(k, 2, "e4m3").transpose(0, 2, 1)
    qn = np.sqrt((q * q).sum(-1))
    kn = np.sqrt((k * k).sum(-1))
    cos = dot / np.maximum(qn[:, :, None] * kn[:, None, :], EPS)
    sq = np.maximum(qn[:, :, None] ** 2 + kn[:, None, :] ** 2 - 2.0 * dot, 0.0)
    euc = -np.sqrt(sq)
    w = softmax(f64(scoring_weights))
    scores = w[0] * dot + w[1] * cos + w[2] * euc
    return softmax(scores)

@@ -1,0 +1,332 @@
+from contextlib import ExitStack
+
+import concourse.mybir as mybir
+from concourse.masks import make_identity
+
+FLOPS = 2 * (2 * 1024 * 512 * 512) + 2 * 2 * 512 * 512 * 512
+
+F32 = mybir.dt.float32
+BF16 = mybir.dt.bfloat16
+U32 = mybir.dt.uint32
+U8 = mybir.dt.uint8
+FP8X4 = mybir.dt.float8_e4m3fn_x4
+ACT = mybir.ActivationFunctionType
+ALU = mybir.AluOpType
+AX = mybir.AxisListType
+
+P = 128
+TINY = 1e-30
+BUFS = {"tp":2,"tq":2,"pj":2,"dt":2,"f":3,"gq":2,"gp":8,"junk":2}
+
+
+def tile_adaptiveattention_pa_kernel(tc, query, key, Wq, bq, Wk, bk, scoring_weights, out):
+    nc = tc.nc
+    with ExitStack() as ctx:
+        ctx.enter_context(tc.manual_schedule())
+        keep = ctx.enter_context(tc.tile_pool(name="keep", bufs=1))
+        work = ctx.enter_context(tc.tile_pool(name="work", bufs=2))
+        psum = ctx.enter_context(tc.psum_pool(name="psum", bufs=1))
+
+        def bank(name, tag):
+            return psum.tile([P, 512], F32, name=name, tag=tag, bufs=BUFS[tag])
+
+        def ew_copy(eng, dst, src):
+            if eng == "s":
+                nc.scalar.copy(out=dst, in_=src)
+            else:
+                nc.vector.tensor_copy(out=dst, in_=src)
+
+        sw_b = keep.tile([P, 3], BF16, name="sw_b")
+        bias_b = [keep.tile([P, 4], BF16, name="bias_b%d" % s) for s in range(2)]
+        nc.scalar.dma_start(out=sw_b[:], in_=scoring_weights.partition_broadcast(P))
+        nc.scalar.dma_start(out=bias_b[0][:], in_=bk.rearrange("(p t) -> p t", t=4))
+        nc.scalar.dma_start(out=bias_b[1][:], in_=bq.rearrange("(p t) -> p t", t=4))
+
+        def w_src(w, h):
+            return w.rearrange("(p t) i -> p t i", t=4)[:, 2 * h : 2 * h + 2, :]
+
+        def k_src(b, h):
+            return key[b, 256 * h : 256 * h + 256, :].rearrange("(n p) i -> p n i", p=P)
+
+        def q_src(b, h):
+            return query[b].rearrange("(p n) i -> p n i", n=4)[:, 2 * h : 2 * h + 2, :]
+
+        srcs = [w_src(Wk, 0), w_src(Wk, 1), k_src(0, 0), k_src(0, 1),
+                w_src(Wq, 0), w_src(Wq, 1), q_src(0, 0), q_src(0, 1),
+                k_src(1, 0), k_src(1, 1), q_src(1, 0), q_src(1, 1)]
+        xs = []
+        for i in range(12):
+            x = keep.tile([P, 1024], BF16, name="xs%d" % i)
+            nc.sync.dma_start(out=x[:].rearrange("p (n i) -> p n i", n=2), in_=srcs[i])
+            xs.append(x)
+
+        ident = keep.tile([P, P], F32, name="ident")
+        make_identity(nc, ident[:])
+        mhalf = keep.tile([P, 4], F32, name="mhalf")
+        nc.vector.memset(mhalf[:], -0.5)
+
+        bias_f = [keep.tile([P, 4], F32, name="bias_f%d" % s) for s in range(2)]
+        wf = keep.tile([P, 3], F32, name="wf")
+        wmax = keep.tile([P, 1], F32, name="wmax")
+        wd = keep.tile([P, 3], F32, name="wd")
+        nc.gpsimd.tensor_copy(out=wf[:], in_=sw_b[:])
+        nc.gpsimd.tensor_scalar(out=wmax[:], in0=wf[:, 0:1], scalar1=wf[:, 1:2], scalar2=wf[:, 2:3],
+                                op0=ALU.max, op1=ALU.max)
+        nc.gpsimd.tensor_scalar(out=wd[:], in0=wf[:], scalar1=wmax[:, 0:1], scalar2=0.0,
+                                op0=ALU.subtract, op1=ALU.add)
+        nc.gpsimd.tensor_copy(out=bias_f[0][:], in_=bias_b[0][:])
+        nc.gpsimd.tensor_copy(out=bias_f[1][:], in_=bias_b[1][:])
+
+        we = keep.tile([P, 3], F32, name="we")
+        wsum = keep.tile([P, 1], F32, name="wsum")
+        rws = keep.tile([P, 1], F32, name="rws")
+        cst = keep.tile([P, 8], F32, name="cst")
+        W0, W1, W2, W2SQ, M2W2, CC = 0, 1, 2, 3, 4, 5
+
+        def col(c):
+            return cst[:, c : c + 1]
+
+        def EXPW():
+            nc.scalar.activation(out=we[:], in_=wd[:], func=ACT.Exp, accum_out=wsum[:])
+
+        def WC():
+            nc.vector.reciprocal(out=rws[:], in_=wsum[:])
+            nc.vector.tensor_scalar(out=cst[:, 0:3], in0=we[:], scalar1=rws[:, 0:1], scalar2=None, op0=ALU.mult)
+            nc.vector.tensor_tensor(out=col(W2SQ), in0=col(W2), in1=col(W2), op=ALU.mult)
+            nc.vector.tensor_scalar(out=col(M2W2), in0=col(W2SQ), scalar1=-2.0, scalar2=None, op0=ALU.mult)
+            nc.vector.tensor_scalar(out=col(CC), in0=col(W1), scalar1=1e8, scalar2=col(W0),
+                                    op0=ALU.mult, op1=ALU.add)
+
+        in_c = [keep.tile([P, 512], U32, name="in_c%d" % o, align_bytes=64) for o in range(6)]
+        in_s = [keep.tile([P, 512], U8, name="in_s%d" % o, align_bytes=64) for o in range(6)]
+        xt = {}
+        grp = {}
+
+        def T(i):
+            t = bank("xt%d" % i, "tp")
+            xw = xs[i][:].bitcast(F32)
+            for nn in range(2):
+                for u in range(2):
+                    nc.tensor.transpose(t[:, u * 256 + nn * 128 : u * 256 + nn * 128 + 128],
+                                        xw[:, nn * 256 + u * 128 : nn * 256 + u * 128 + 128], ident[:])
+            xt[i] = t
+
+        def EV(i, eng):
+            g = keep.tile([P, 1024], BF16, name="grp%d" % i, align_bytes=64)
+            ew_copy(eng, g[:].bitcast(F32).rearrange("p (r u) -> p r u", u=2),
+                    xt[i][:].rearrange("p (u r) -> p r u", u=2))
+            grp[i] = g
+
+        def QZ(i):
+            o, h = i // 2, i % 2
+            nc.vector.quantize_mx(out=in_c[o][:, 256 * h : 256 * h + 256].bitcast(FP8X4),
+                                  scales=in_s[o][:, 256 * h : 256 * h + 256], in_=grp[i][:])
+
+        g_w = [0, 2, 0, 2]
+        g_x = [1, 3, 4, 5]
+        pj = {}
+        ft = {}
+        gq = {}
+        qk_c = [keep.tile([P, 512], U32, name="qk_c%d" % g, align_bytes=64) for g in range(4)]
+        qk_s = [keep.tile([P, 512], U8, name="qk_s%d" % g, align_bytes=64) for g in range(4)]
+
+        def PJ(g, t):
+            a = bank("pj%d_%d" % (g, t), "pj")
+            nc.tensor.matmul_mx(out=a[:],
+                                lhsT=in_c[g_w[g]][:, t * 128 : t * 128 + 128].bitcast(FP8X4),
+                                lhsT_scale=in_s[g_w[g]][:, t * 128 : t * 128 + 128],
+                                rhs=in_c[g_x[g]][:].bitcast(FP8X4), rhs_scale=in_s[g_x[g]][:],
+                                start=True, stop=True)
+            pj[(g, t)] = a
+
+        def TH(g, t):
+            if g not in ft:
+                ft[g] = work.tile([P, 2048], F32, name="f%d" % g, tag="f", bufs=BUFS["f"])
+            nc.scalar.activation(out=ft[g][:, t * 512 : t * 512 + 512], in_=pj[(g, t)][:], func=ACT.Tanh,
+                                 bias=bias_f[g % 2][:, t : t + 1], scale=1.0)
+
+        def RG(g):
+            r = work.tile([P, 2048], BF16, name="gq%d" % g, tag="gq", bufs=BUFS["gq"], align_bytes=64)
+            nc.vector.tensor_copy(out=r[:].rearrange("p (w t) -> p w t", t=4),
+                                  in_=ft[g][:].rearrange("p (t w) -> p w t", t=4))
+            gq[g] = r
+
+        def QG(g):
+            nc.vector.quantize_mx(out=qk_c[g][:].bitcast(FP8X4), scales=qk_s[g][:], in_=gq[g][:])
+
+        tq = {}
+        n2 = [keep.tile([P, 4], F32, name="n2_%d" % g) for g in range(4)]
+        n2c = [keep.tile([P, 4], F32, name="n2c%d" % g) for g in range(4)]
+        n2w = [keep.tile([P, 4], F32, name="n2w%d" % g) for g in range(4)]
+        rn = [keep.tile([P, 4], F32, name="rn%d" % g) for g in range(4)]
+        w1rq = [keep.tile([P, 4], F32, name="w1rq%d" % b) for b in range(2)]
+
+        def TQ(g, n):
+            a = bank("tq%d_%d" % (g, n), "tq")
+            for t in range(4):
+                nc.tensor.transpose(a[:, t * 128 : t * 128 + 128],
+                                    ft[g][:, t * 512 + n * 128 : t * 512 + n * 128 + 128], ident[:])
+            tq[(g, n)] = a
+
+        def SQ(g, n):
+            j = work.tile([P, 512], BF16, name="jk%d_%d" % (g, n), tag="junk", bufs=BUFS["junk"])
+            nc.scalar.activation(out=j[:], in_=tq[(g, n)][:], func=ACT.Square, accum_out=n2[g][:, n : n + 1])
+
+        def NC(g):
+            nc.vector.tensor_scalar(out=n2c[g][:], in0=n2[g][:], scalar1=TINY, scalar2=None, op0=ALU.max)
+            nc.vector.tensor_scalar(out=n2w[g][:], in0=n2[g][:], scalar1=TINY, scalar2=col(W2SQ),
+                                    op0=ALU.max, op1=ALU.mult)
+
+        def PW(g):
+            nc.gpsimd.tensor_tensor(out=rn[g][:], in0=n2c[g][:], in1=mhalf[:], op=ALU.pow)
+            if g % 2 == 1:
+                nc.gpsimd.tensor_scalar(out=w1rq[g // 2][:], in0=rn[g][:], scalar1=col(W1), scalar2=0.0,
+                                        op0=ALU.mult, op1=ALU.add)
+
+        kn2w_sb = [keep.tile([P, 512], F32, name="kn2w_sb%d" % b) for b in range(2)]
+        rkb_sb = [keep.tile([P, 512], F32, name="rkb_sb%d" % b) for b in range(2)]
+        bc = {}
+
+        def spread(name, v):
+            a = bank(name, "tq")
+            for n in range(4):
+                nc.tensor.transpose(a[:, n * 128 : n * 128 + 128], v[:, n : n + 1].to_broadcast([P, P]), ident[:])
+            return a
+
+        def BK(b):
+            bc[("k", b)] = spread("bck%d" % b, n2w[2 * b])
+
+        def BR(b):
+            bc[("r", b)] = spread("bcr%d" % b, rn[2 * b])
+
+        def CK(b, eng):
+            ew_copy(eng, kn2w_sb[b][:], bc[("k", b)][:])
+
+        def CR(b, eng):
+            ew_copy(eng, rkb_sb[b][:], bc[("r", b)][:])
+
+        dot = {}
+        zt = {}
+        gp = {}
+        t2 = {}
+        mn = {}
+        ssum = {}
+        rs = {}
+
+        def D(b, n, tag="dt"):
+            a = bank("dot%d_%d" % (b, n), tag)
+            nc.tensor.matmul_mx(out=a[:],
+                                lhsT=qk_c[2 * b + 1][:, n * 128 : n * 128 + 128].bitcast(FP8X4),
+                                lhsT_scale=qk_s[2 * b + 1][:, n * 128 : n * 128 + 128],
+                                rhs=qk_c[2 * b][:].bitcast(FP8X4), rhs_scale=qk_s[2 * b][:],
+                                start=True, stop=True)
+            dot[(b, n)] = a
+
+        def A(b, n):
+            z = work.tile([P, 512], F32, name="z%d_%d" % (b, n), tag="z", bufs=8)
+            nc.vector.scalar_tensor_tensor(out=z[:], in0=dot[(b, n)][:], scalar=col(M2W2), in1=kn2w_sb[b][:],
+                                           op0=ALU.mult, op1=ALU.add)
+            zt[(b, n)] = z
+
+        def B(b, n):
+            z = zt[(b, n)]
+            nc.vector.tensor_scalar(out=z[:], in0=z[:], scalar1=n2w[2 * b + 1][:, n : n + 1], scalar2=TINY,
+                                    op0=ALU.add, op1=ALU.max)
+
+        def C(b, n):
+            z = zt[(b, n)]
+            nc.scalar.activation(out=z[:], in_=z[:], func=ACT.Sqrt)
+
+        def DG(b, n, eng="g"):
+            g = work.tile([P, 512], F32, name="gp%d_%d" % (b, n), tag="gp", bufs=BUFS["gp"])
+            if eng == "g":
+                nc.gpsimd.tensor_scalar(out=g[:], in0=rkb_sb[b][:], scalar1=w1rq[b][:, n : n + 1], scalar2=col(W0),
+                                        op0=ALU.mult, op1=ALU.add)
+            elif eng == "v":
+                nc.vector.tensor_scalar(out=g[:], in0=rkb_sb[b][:], scalar1=w1rq[b][:, n : n + 1], scalar2=col(W0),
+                                        op0=ALU.mult, op1=ALU.add)
+            else:
+                nc.scalar.activation(out=g[:], in_=rkb_sb[b][:], func=ACT.Identity, bias=col(W0),
+                                     scale=w1rq[b][:, n : n + 1])
+            gp[(b, n)] = g
+
+        def E(b, n):
+            t = work.tile([P, 512], F32, name="t2_%d_%d" % (b, n), tag="t2", bufs=8)
+            nc.vector.scalar_tensor_tensor(out=t[:], in0=gp[(b, n)][:], scalar=col(CC), in1=dot[(b, n)][:],
+                                           op0=ALU.min, op1=ALU.mult)
+            t2[(b, n)] = t
+
+        def F(b, n, eng="v"):
+            t = t2[(b, n)]
+            if eng == "g":
+                nc.gpsimd.tensor_tensor(out=t[:], in0=zt[(b, n)][:], in1=t[:], op=ALU.subtract)
+            else:
+                nc.vector.tensor_tensor(out=t[:], in0=zt[(b, n)][:], in1=t[:], op=ALU.subtract)
+
+        def M(b, n, eng="v"):
+            m = work.tile([P, 1], F32, name="mn%d_%d" % (b, n), tag="mn", bufs=8)
+            nc.vector.tensor_reduce(out=m[:], in_=t2[(b, n)][:], axis=AX.X, op=ALU.min)
+            mn[(b, n)] = m
+
+        def H(b, n):
+            t = t2[(b, n)]
+            s = work.tile([P, 1], F32, name="ss%d_%d" % (b, n), tag="ss", bufs=8)
+            nc.scalar.activation(out=t[:], in_=t[:], func=ACT.Exp, bias=mn[(b, n)][:, 0:1], scale=-1.0,
+                                 accum_out=s[:])
+            ssum[(b, n)] = s
+
+        def R(b, n):
+            r = work.tile([P, 1], F32, name="rs%d_%d" % (b, n), tag="rs", bufs=8)
+            nc.vector.reciprocal(out=r[:], in_=ssum[(b, n)][:])
+            rs[(b, n)] = r
+
+        def I(b, n, eng):
+            t = t2[(b, n)]
+            r = rs[(b, n)]
+            if eng == "s":
+                nc.scalar.activation(out=t[:], in_=t[:], func=ACT.Copy, scale=r[:, 0:1])
+            elif eng == "g":
+                nc.gpsimd.tensor_scalar(out=t[:], in0=t[:], scalar1=r[:, 0:1], scalar2=0.0, op0=ALU.mult, op1=ALU.add)
+            else:
+                nc.vector.tensor_scalar(out=t[:], in0=t[:], scalar1=r[:, 0:1], scalar2=None, op0=ALU.mult)
+
+        def ST(b, n):
+            nc.sync.dma_start(out=out[b].rearrange("(r n) j -> r n j", n=4)[:, n, :], in_=t2[(b, n)][:])
+
+        T(0); T(1); EV(0, "s"); EXPW(); EV(1, "s"); QZ(0)
+        T(2); T(3); EV(2, "s"); EV(3, "s"); QZ(2); T(5)
+        QZ(1); T(4); QZ(3); EV(5, "s"); PJ(0, 0); EV(4, "s")
+        QZ(5); T(6); TH(0, 0); QZ(4); T(7); EV(6, "v")
+        PJ(0, 2); PJ(0, 1); EV(7, "v"); TH(0, 2); T(10); TH(0, 1)
+        QZ(7); PJ(0, 3); QZ(6); T(9); TH(0, 3); WC()
+        PJ(1, 0); EV(10, "v"); PJ(1, 3); TH(1, 0); TQ(0, 0); EV(9, "v")
+        TH(1, 3); PJ(1, 1); QZ(10); T(8); SQ(0, 0); QZ(9)
+        PJ(1, 2); TH(1, 1); EV(8, "v"); TQ(0, 1); TH(1, 2); TQ(0, 2)
+        QZ(8); SQ(0, 1); RG(0); PJ(2, 0); PJ(2, 1); SQ(0, 2)
+        TQ(0, 3); RG(1); TH(2, 0); TQ(1, 3); SQ(0, 3); PJ(2, 3)
+        QG(0); T(11); TH(2, 1); QG(1); SQ(1, 3); PJ(2, 2)
+        TQ(1, 0); EV(11, "v"); TH(2, 2); TQ(1, 1); TH(2, 3); QZ(11)
+        D(0, 1); NC(0); SQ(1, 0); RG(2); D(0, 0); PW(0)
+        PJ(3, 2); SQ(1, 1); TQ(1, 2); TH(3, 2); BK(0); QG(2)
+        SQ(1, 2); PJ(3, 1); CK(0, "v"); PJ(3, 3); TH(3, 1); BR(0)
+        NC(1); A(0, 1); TH(3, 3); PW(1); PJ(3, 0); TQ(2, 3)
+        CR(0, "v"); TH(3, 0); A(0, 0); SQ(2, 3); TQ(3, 2); RG(3)
+        DG(0, 1); TQ(2, 1); SQ(3, 2); SQ(2, 1); TQ(2, 2); DG(0, 0)
+        B(0, 1); E(0, 1); TQ(3, 1); SQ(2, 2); QG(3); DG(0, 3)
+        SQ(3, 1); TQ(2, 0); E(0, 0); DG(0, 2); D(0, 3); B(0, 0)
+        SQ(2, 0); TQ(3, 3); A(0, 3); TQ(3, 0); SQ(3, 3); NC(2)
+        B(0, 3); PW(2); D(0, 2); E(0, 3); SQ(3, 0); BK(1)
+        A(0, 2); C(0, 1); D(1, 1); BR(1); NC(3); B(0, 2)
+        PW(3); E(0, 2); CR(1, "v"); D(1, 0); C(0, 3); F(0, 1, "v")
+        DG(1, 1); C(0, 2); CK(1, "v"); M(0, 1); DG(1, 3); E(1, 1)
+        H(0, 1); DG(1, 0); A(1, 1); A(1, 0); D(1, 3); DG(1, 2)
+        E(1, 0); C(0, 0); B(1, 0); D(1, 2); A(1, 3); R(0, 1)
+        B(1, 1); B(1, 3); F(0, 3, "v"); C(1, 0); A(1, 2); C(1, 3)
+        F(1, 0, "v"); I(0, 1, "s"); B(1, 2); C(1, 1); M(1, 0); C(1, 2)
+        M(0, 3); H(1, 0); F(0, 2, "v"); F(0, 0, "v"); M(0, 2); M(0, 0)
+        H(0, 3); E(1, 2); H(0, 0); E(1, 3); H(0, 2); R(1, 0)
+        R(0, 0); F(1, 3, "v"); I(1, 0, "s"); R(0, 2); F(1, 2, "v"); ST(1, 0)
+        I(0, 2, "s"); R(0, 3); M(1, 3); I(0, 0, "s"); ST(0, 2); I(0, 3, "s")
+        F(1, 1, "v"); H(1, 3); M(1, 2); ST(0, 3); ST(0, 1); ST(0, 0)
+        M(1, 1); H(1, 2); R(1, 3); H(1, 1); R(1, 2); I(1, 3, "v")
+        I(1, 2, "s"); ST(1, 3); R(1, 1); I(1, 1, "s"); ST(1, 2); ST(1, 1)

@@ -54,11 +54,11 @@ def tile_adaptiveattention_pa_kernel(tc, query, key, Wq, bq, Wk, bk, scoring_wei
         srcs = [w_src(Wk, 0), w_src(Wk, 1), k_src(0, 0), k_src(0, 1),
                 w_src(Wq, 0), w_src(Wq, 1), q_src(0, 0), q_src(0, 1),
                 k_src(1, 0), k_src(1, 1), q_src(1, 0), q_src(1, 1)]
-        xs = []
-        for i in range(12):
+        xs = {}
+        for i in [0,2,3,1,4,6,7,5,8,9,10,11]:
             x = keep.tile([P, 1024], BF16, name="xs%d" % i)
             nc.sync.dma_start(out=x[:].rearrange("p (n i) -> p n i", n=2), in_=srcs[i])
-            xs.append(x)
+            xs[i] = x
 
         ident = keep.tile([P, P], F32, name="ident")
         make_identity(nc, ident[:])
@@ -263,7 +263,7 @@ def tile_adaptiveattention_pa_kernel(tc, query, key, Wq, bq, Wk, bk, scoring_wei
             else:
                 nc.vector.tensor_tensor(out=t[:], in0=zt[(b, n)][:], in1=t[:], op=ALU.subtract)
 
-        def M(b, n, eng="v"):
+        def M(b, n):
             m = work.tile([P, 1], F32, name="mn%d_%d" % (b, n), tag="mn", bufs=8)
             nc.vector.tensor_reduce(out=m[:], in_=t2[(b, n)][:], axis=AX.X, op=ALU.min)
             mn[(b, n)] = m
@@ -293,40 +293,40 @@ def tile_adaptiveattention_pa_kernel(tc, query, key, Wq, bq, Wk, bk, scoring_wei
         def ST(b, n):
             nc.sync.dma_start(out=out[b].rearrange("(r n) j -> r n j", n=4)[:, n, :], in_=t2[(b, n)][:])
 
-        T(0); T(1); EV(0, "s"); EXPW(); EV(1, "s"); QZ(0)
-        T(2); T(3); EV(2, "s"); EV(3, "s"); QZ(2); T(5)
-        QZ(1); T(4); QZ(3); EV(5, "s"); PJ(0, 0); EV(4, "s")
-        QZ(5); T(6); TH(0, 0); QZ(4); T(7); EV(6, "v")
-        PJ(0, 2); PJ(0, 1); EV(7, "v"); TH(0, 2); T(10); TH(0, 1)
-        QZ(7); PJ(0, 3); QZ(6); T(9); TH(0, 3); WC()
-        PJ(1, 0); EV(10, "v"); PJ(1, 3); TH(1, 0); TQ(0, 0); EV(9, "v")
-        TH(1, 3); PJ(1, 1); QZ(10); T(8); SQ(0, 0); QZ(9)
-        PJ(1, 2); TH(1, 1); EV(8, "v"); TQ(0, 1); TH(1, 2); TQ(0, 2)
-        QZ(8); SQ(0, 1); RG(0); PJ(2, 0); PJ(2, 1); SQ(0, 2)
-        TQ(0, 3); RG(1); TH(2, 0); TQ(1, 3); SQ(0, 3); PJ(2, 3)
-        QG(0); T(11); TH(2, 1); QG(1); SQ(1, 3); PJ(2, 2)
-        TQ(1, 0); EV(11, "v"); TH(2, 2); TQ(1, 1); TH(2, 3); QZ(11)
-        D(0, 1); NC(0); SQ(1, 0); RG(2); D(0, 0); PW(0)
-        PJ(3, 2); SQ(1, 1); TQ(1, 2); TH(3, 2); BK(0); QG(2)
-        SQ(1, 2); PJ(3, 1); CK(0, "v"); PJ(3, 3); TH(3, 1); BR(0)
-        NC(1); A(0, 1); TH(3, 3); PW(1); PJ(3, 0); TQ(2, 3)
-        CR(0, "v"); TH(3, 0); A(0, 0); SQ(2, 3); TQ(3, 2); RG(3)
-        DG(0, 1); TQ(2, 1); SQ(3, 2); SQ(2, 1); TQ(2, 2); DG(0, 0)
-        B(0, 1); E(0, 1); TQ(3, 1); SQ(2, 2); QG(3); DG(0, 3)
-        SQ(3, 1); TQ(2, 0); E(0, 0); DG(0, 2); D(0, 3); B(0, 0)
-        SQ(2, 0); TQ(3, 3); A(0, 3); TQ(3, 0); SQ(3, 3); NC(2)
-        B(0, 3); PW(2); D(0, 2); E(0, 3); SQ(3, 0); BK(1)
-        A(0, 2); C(0, 1); D(1, 1); BR(1); NC(3); B(0, 2)
-        PW(3); E(0, 2); CR(1, "v"); D(1, 0); C(0, 3); F(0, 1, "v")
-        DG(1, 1); C(0, 2); CK(1, "v"); M(0, 1); DG(1, 3); E(1, 1)
-        H(0, 1); DG(1, 0); A(1, 1); A(1, 0); D(1, 3); DG(1, 2)
-        E(1, 0); C(0, 0); B(1, 0); D(1, 2); A(1, 3); R(0, 1)
-        B(1, 1); B(1, 3); F(0, 3, "v"); C(1, 0); A(1, 2); C(1, 3)
-        F(1, 0, "v"); I(0, 1, "s"); B(1, 2); C(1, 1); M(1, 0); C(1, 2)
-        M(0, 3); H(1, 0); F(0, 2, "v"); F(0, 0, "v"); M(0, 2); M(0, 0)
-        H(0, 3); E(1, 2); H(0, 0); E(1, 3); H(0, 2); R(1, 0)
-        R(0, 0); F(1, 3, "v"); I(1, 0, "s"); R(0, 2); F(1, 2, "v"); ST(1, 0)
-        I(0, 2, "s"); R(0, 3); M(1, 3); I(0, 0, "s"); ST(0, 2); I(0, 3, "s")
-        F(1, 1, "v"); H(1, 3); M(1, 2); ST(0, 3); ST(0, 1); ST(0, 0)
-        M(1, 1); H(1, 2); R(1, 3); H(1, 1); R(1, 2); I(1, 3, "v")
-        I(1, 2, "s"); ST(1, 3); R(1, 1); I(1, 1, "s"); ST(1, 2); ST(1, 1)
+        T(0); T(2); EV(0, "s"); EV(2, "s"); T(3); EXPW()
+        T(1); WC(); EV(3, "s"); QZ(0); EV(1, "s"); QZ(3)
+        T(4); QZ(2); T(7); EV(4, "s"); PJ(0, 1); EV(7, "s")
+        QZ(4); T(6); QZ(1); TH(0, 1); PJ(0, 0); QZ(7)
+        T(8); EV(6, "s"); PJ(0, 2); TH(0, 0); EV(8, "v"); T(5)
+        TH(0, 2); PJ(0, 3); QZ(8); EV(5, "s"); T(9); QZ(6)
+        TH(0, 3); PJ(1, 1); QZ(5); EV(9, "v"); TH(1, 1); PJ(1, 3)
+        TQ(0, 0); TH(1, 3); QZ(9); PJ(1, 2); RG(0); SQ(0, 0)
+        PJ(1, 0); TQ(0, 2); TH(1, 2); T(10); QG(0); TH(1, 0)
+        PJ(2, 0); SQ(0, 2); EV(10, "v"); TQ(1, 0); TH(2, 0); RG(1)
+        TQ(1, 2); SQ(1, 0); PJ(2, 1); PJ(2, 2); SQ(1, 2); TQ(0, 3)
+        TH(2, 1); T(11); SQ(0, 3); TQ(0, 1); EV(11, "v"); TH(2, 2)
+        PJ(2, 3); QG(1); TQ(1, 3); SQ(0, 1); QZ(11); TH(2, 3)
+        QZ(10); TQ(1, 1); NC(0); SQ(1, 3); RG(2); PJ(3, 1)
+        PW(0); PJ(3, 2); SQ(1, 1); BK(0); TH(3, 1); D(0, 0)
+        NC(1); BR(0); PW(1); CK(0, "s"); PJ(3, 0); TH(3, 2)
+        A(0, 0); TQ(2, 3); CR(0, "s"); QG(2); D(0, 3); PJ(3, 3)
+        TH(3, 0); DG(0, 0, "g"); TQ(2, 2); A(0, 3); SQ(2, 3); B(0, 3)
+        SQ(2, 2); DG(0, 3, "g"); TQ(2, 0); E(0, 0); TH(3, 3); TQ(2, 1)
+        B(0, 0); DG(0, 1, "g"); SQ(2, 0); E(0, 3); D(0, 2); SQ(2, 1)
+        RG(3); TQ(3, 3); DG(0, 2, "g"); TQ(3, 2); SQ(3, 3); NC(2)
+        A(0, 2); D(0, 1); PW(2); SQ(3, 2); TQ(3, 0); E(0, 1)
+        TQ(3, 1); SQ(3, 0); E(0, 2); SQ(3, 1); QG(3); BK(1)
+        BR(1); NC(3); CK(1, "s"); A(0, 1); PW(3); D(1, 0)
+        CR(1, "s"); B(0, 2); D(1, 2); B(0, 1); A(1, 0); C(0, 1)
+        DG(1, 0, "g"); A(1, 2); B(1, 0); B(1, 2); DG(1, 2, "g"); E(1, 0)
+        D(1, 1); DG(1, 1, "g"); C(0, 0); E(1, 2); C(1, 2); F(0, 1, "v")
+        D(1, 3); F(0, 0, "g"); C(0, 2); A(1, 1); C(1, 0); A(1, 3)
+        C(0, 3); F(1, 0, "g"); B(1, 1); B(1, 3); C(1, 1); M(0, 0)
+        C(1, 3); F(0, 3, "v"); F(0, 2, "g"); H(0, 0); M(0, 1); M(1, 0)
+        DG(1, 3, "g"); M(0, 3); M(0, 2); H(0, 3); E(1, 3); H(1, 0)
+        R(0, 0); F(1, 2, "v"); I(0, 0, "g"); H(0, 1); R(0, 3); F(1, 3, "v")
+        H(0, 2); I(0, 3, "g"); R(1, 0); ST(0, 0); E(1, 1); R(0, 1)
+        M(1, 2); I(0, 1, "g"); ST(0, 3); R(0, 2); F(1, 1, "v"); H(1, 2)
+        I(0, 2, "g"); I(1, 0, "v"); ST(0, 1); M(1, 1); ST(1, 0); R(1, 2)
+        M(1, 3); H(1, 1); ST(0, 2); I(1, 2, "v"); H(1, 3); R(1, 1)
+        ST(1, 2); I(1, 1, "v"); R(1, 3); ST(1, 1); I(1, 3, "v"); ST(1, 3)

@@ -28,7 +28,7 @@ def tile_adaptiveattention_pa_kernel(tc, query, key, Wq, bq, Wk, bk, scoring_wei
         psum = ctx.enter_context(tc.psum_pool(name="psum", bufs=1))
 
         def bank(name, tag):
-            return psum.tile([P, 512], F32, name=name, tag=tag, bufs=BUFS[tag])
+            return psum.tile([P, 512], F32, name=name, tag="ps", bufs=8)
 
         def ew_copy(eng, dst, src):
             if eng == "s":
@@ -293,40 +293,40 @@ def tile_adaptiveattention_pa_kernel(tc, query, key, Wq, bq, Wk, bk, scoring_wei
         def ST(b, n):
             nc.sync.dma_start(out=out[b].rearrange("(r n) j -> r n j", n=4)[:, n, :], in_=t2[(b, n)][:])
 
-        T(0); T(2); EV(0, "s"); EV(2, "s"); T(3); EXPW()
-        T(1); WC(); EV(3, "s"); QZ(0); EV(1, "s"); QZ(3)
-        T(4); QZ(2); T(7); EV(4, "s"); PJ(0, 1); EV(7, "s")
-        QZ(4); T(6); QZ(1); TH(0, 1); PJ(0, 0); QZ(7)
-        T(8); EV(6, "s"); PJ(0, 2); TH(0, 0); EV(8, "v"); T(5)
-        TH(0, 2); PJ(0, 3); QZ(8); EV(5, "s"); T(9); QZ(6)
-        TH(0, 3); PJ(1, 1); QZ(5); EV(9, "v"); TH(1, 1); PJ(1, 3)
-        TQ(0, 0); TH(1, 3); QZ(9); PJ(1, 2); RG(0); SQ(0, 0)
-        PJ(1, 0); TQ(0, 2); TH(1, 2); T(10); QG(0); TH(1, 0)
-        PJ(2, 0); SQ(0, 2); EV(10, "v"); TQ(1, 0); TH(2, 0); RG(1)
-        TQ(1, 2); SQ(1, 0); PJ(2, 1); PJ(2, 2); SQ(1, 2); TQ(0, 3)
-        TH(2, 1); T(11); SQ(0, 3); TQ(0, 1); EV(11, "v"); TH(2, 2)
-        PJ(2, 3); QG(1); TQ(1, 3); SQ(0, 1); QZ(11); TH(2, 3)
-        QZ(10); TQ(1, 1); NC(0); SQ(1, 3); RG(2); PJ(3, 1)
-        PW(0); PJ(3, 2); SQ(1, 1); BK(0); TH(3, 1); D(0, 0)
-        NC(1); BR(0); PW(1); CK(0, "s"); PJ(3, 0); TH(3, 2)
-        A(0, 0); TQ(2, 3); CR(0, "s"); QG(2); D(0, 3); PJ(3, 3)
-        TH(3, 0); DG(0, 0, "g"); TQ(2, 2); A(0, 3); SQ(2, 3); B(0, 3)
-        SQ(2, 2); DG(0, 3, "g"); TQ(2, 0); E(0, 0); TH(3, 3); TQ(2, 1)
-        B(0, 0); DG(0, 1, "g"); SQ(2, 0); E(0, 3); D(0, 2); SQ(2, 1)
-        RG(3); TQ(3, 3); DG(0, 2, "g"); TQ(3, 2); SQ(3, 3); NC(2)
-        A(0, 2); D(0, 1); PW(2); SQ(3, 2); TQ(3, 0); E(0, 1)
-        TQ(3, 1); SQ(3, 0); E(0, 2); SQ(3, 1); QG(3); BK(1)
-        BR(1); NC(3); CK(1, "s"); A(0, 1); PW(3); D(1, 0)
-        CR(1, "s"); B(0, 2); D(1, 2); B(0, 1); A(1, 0); C(0, 1)
-        DG(1, 0, "g"); A(1, 2); B(1, 0); B(1, 2); DG(1, 2, "g"); E(1, 0)
-        D(1, 1); DG(1, 1, "g"); C(0, 0); E(1, 2); C(1, 2); F(0, 1, "v")
-        D(1, 3); F(0, 0, "g"); C(0, 2); A(1, 1); C(1, 0); A(1, 3)
-        C(0, 3); F(1, 0, "g"); B(1, 1); B(1, 3); C(1, 1); M(0, 0)
-        C(1, 3); F(0, 3, "v"); F(0, 2, "g"); H(0, 0); M(0, 1); M(1, 0)
-        DG(1, 3, "g"); M(0, 3); M(0, 2); H(0, 3); E(1, 3); H(1, 0)
-        R(0, 0); F(1, 2, "v"); I(0, 0, "g"); H(0, 1); R(0, 3); F(1, 3, "v")
-        H(0, 2); I(0, 3, "g"); R(1, 0); ST(0, 0); E(1, 1); R(0, 1)
-        M(1, 2); I(0, 1, "g"); ST(0, 3); R(0, 2); F(1, 1, "v"); H(1, 2)
-        I(0, 2, "g"); I(1, 0, "v"); ST(0, 1); M(1, 1); ST(1, 0); R(1, 2)
-        M(1, 3); H(1, 1); ST(0, 2); I(1, 2, "v"); H(1, 3); R(1, 1)
-        ST(1, 2); I(1, 1, "v"); R(1, 3); ST(1, 1); I(1, 3, "v"); ST(1, 3)
+        T(0); T(2); EV(0, "s"); T(3); EV(2, "s"); T(1)
+        EV(3, "s"); QZ(2); T(4); EXPW(); EV(1, "s"); QZ(3)
+        T(6); EV(4, "s"); QZ(1); T(7); QZ(0); EV(6, "s")
+        QZ(4); T(5); WC(); EV(7, "s"); QZ(6); PJ(0, 3)
+        EV(5, "s"); QZ(7); PJ(0, 1); PJ(0, 2); TH(0, 3); QZ(5)
+        PJ(0, 0); T(9); TH(0, 2); T(8); TH(0, 1); EV(9, "v")
+        PJ(1, 2); TH(0, 0); PJ(1, 0); QZ(9); PJ(1, 3); TH(1, 2)
+        EV(8, "v"); PJ(1, 1); T(11); TH(1, 0); QZ(8); TH(1, 3)
+        T(10); EV(11, "v"); TH(1, 1); PJ(2, 2); EV(10, "v"); PJ(2, 0)
+        TH(2, 2); PJ(2, 1); PJ(2, 3); QZ(10); TH(2, 1); TQ(0, 0)
+        RG(1); TH(2, 0); TQ(0, 3); SQ(0, 0); TQ(0, 2); QZ(11)
+        RG(0); SQ(0, 3); TQ(0, 1); SQ(0, 2); PJ(3, 3); PJ(3, 2)
+        QG(1); TH(2, 3); PJ(3, 0); QG(0); SQ(0, 1); PJ(3, 1)
+        TQ(1, 3); RG(2); TH(3, 2); TQ(1, 2); TH(3, 0); TQ(1, 0)
+        NC(0); TH(3, 3); QG(2); PW(0); TQ(1, 1); TH(3, 1)
+        BK(0); SQ(1, 3); RG(3); TQ(2, 2); SQ(1, 2); D(0, 3)
+        SQ(1, 0); QG(3); D(0, 0); BR(0); SQ(1, 1); D(0, 1)
+        CK(0, "s"); NC(1); D(0, 2); TQ(2, 0); PW(1); SQ(2, 2)
+        A(0, 3); TQ(3, 1); CR(0, "s"); A(0, 0); TQ(2, 3); B(0, 3)
+        DG(0, 3, "g"); B(0, 0); C(0, 3); A(0, 1); A(0, 2); DG(0, 0, "g")
+        B(0, 1); E(0, 3); DG(0, 1, "g"); E(0, 0); TQ(2, 1); C(0, 0)
+        DG(0, 2, "g"); F(0, 3, "v"); TQ(3, 0); SQ(2, 0); E(0, 1); D(1, 1)
+        SQ(2, 1); B(0, 2); TQ(3, 2); SQ(2, 3); E(0, 2); C(0, 2)
+        F(0, 0, "v"); TQ(3, 3); SQ(3, 1); NC(2); F(0, 2, "v"); PW(2)
+        BK(1); SQ(3, 0); M(0, 0); D(1, 2); SQ(3, 2); D(1, 3)
+        M(0, 2); D(1, 0); CK(1, "s"); BR(1); M(0, 3); SQ(3, 3)
+        A(1, 2); C(0, 1); NC(3); A(1, 3); CR(1, "s"); PW(3)
+        A(1, 1); B(1, 2); F(0, 1, "v"); DG(1, 2, "g"); B(1, 1); A(1, 0)
+        C(1, 1); DG(1, 0, "g"); B(1, 3); C(1, 2); E(1, 2); C(1, 3)
+        DG(1, 1, "g"); B(1, 0); M(0, 1); C(1, 0); DG(1, 3, "g"); F(1, 2, "v")
+        H(0, 0); E(1, 0); E(1, 3); E(1, 1); M(1, 2); H(0, 1)
+        F(1, 0, "v"); H(0, 3); F(1, 1, "v"); H(1, 2); M(1, 0); H(0, 2)
+        R(0, 3); R(0, 1); R(0, 0); F(1, 3, "v"); H(1, 0); R(1, 2)
+        I(0, 0, "v"); I(0, 1, "v"); ST(0, 0); I(1, 2, "v"); R(1, 0); M(1, 1)
+        ST(1, 2); ST(0, 1); I(1, 0, "v"); H(1, 1); M(1, 3); ST(1, 0)
+        I(0, 3, "v"); H(1, 3); R(0, 2); R(1, 1); ST(0, 3); I(0, 2, "v")
+        I(1, 1, "v"); ST(0, 2); R(1, 3); ST(1, 1); I(1, 3, "v"); ST(1, 3)

@@ -16,7 +16,7 @@ AX = mybir.AxisListType
 
 P = 128
 TINY = 1e-30
-BUFS = {"tp":2,"tq":2,"pj":2,"dt":2,"f":3,"gq":2,"gp":8,"junk":2}
+BUFS = {"f":3,"gq":2,"gp":8,"junk":2}
 
 
 def tile_adaptiveattention_pa_kernel(tc, query, key, Wq, bq, Wk, bk, scoring_weights, out):
@@ -62,6 +62,8 @@ def tile_adaptiveattention_pa_kernel(tc, query, key, Wq, bq, Wk, bk, scoring_wei
 
         ident = keep.tile([P, P], F32, name="ident")
         make_identity(nc, ident[:])
+        nident = keep.tile([P, P], F32, name="nident")
+        nc.gpsimd.tensor_scalar(out=nident[:], in0=ident[:], scalar1=-1.0, scalar2=0.0, op0=ALU.mult, op1=ALU.add)
         mhalf = keep.tile([P, 4], F32, name="mhalf")
         nc.vector.memset(mhalf[:], -0.5)
 
@@ -112,15 +114,14 @@ def tile_adaptiveattention_pa_kernel(tc, query, key, Wq, bq, Wk, bk, scoring_wei
             xt[i] = t
 
         def EV(i, eng):
-            g = keep.tile([P, 1024], BF16, name="grp%d" % i, align_bytes=64)
-            ew_copy(eng, g[:].bitcast(F32).rearrange("p (r u) -> p r u", u=2),
-                    xt[i][:].rearrange("p (u r) -> p r u", u=2))
-            grp[i] = g
-
-        def QZ(i):
             o, h = i // 2, i % 2
-            nc.vector.quantize_mx(out=in_c[o][:, 256 * h : 256 * h + 256].bitcast(FP8X4),
-                                  scales=in_s[o][:, 256 * h : 256 * h + 256], in_=grp[i][:])
+            if o not in grp:
+                grp[o] = keep.tile([P, 2048], BF16, name="grp%d" % o, align_bytes=64)
+            ew_copy(eng, grp[o][:, 1024 * h : 1024 * h + 1024].bitcast(F32).rearrange("p (r u) -> p r u", u=2),
+                    xt[i][:].rearrange("p (u r) -> p r u", u=2))
+
+        def QZ(o):
+            nc.vector.quantize_mx(out=in_c[o][:].bitcast(FP8X4), scales=in_s[o][:], in_=grp[o][:])
 
         g_w = [0, 2, 0, 2]
         g_x = [1, 3, 4, 5]
@@ -172,10 +173,10 @@ def tile_adaptiveattention_pa_kernel(tc, query, key, Wq, bq, Wk, bk, scoring_wei
             j = work.tile([P, 512], BF16, name="jk%d_%d" % (g, n), tag="junk", bufs=BUFS["junk"])
             nc.scalar.activation(out=j[:], in_=tq[(g, n)][:], func=ACT.Square, accum_out=n2[g][:, n : n + 1])
 
-        def NC(g):
-            nc.vector.tensor_scalar(out=n2c[g][:], in0=n2[g][:], scalar1=TINY, scalar2=None, op0=ALU.max)
-            nc.vector.tensor_scalar(out=n2w[g][:], in0=n2[g][:], scalar1=TINY, scalar2=col(W2SQ),
-                                    op0=ALU.max, op1=ALU.mult)
+        def NC(g, eng):
+            e = nc.gpsimd if eng == "g" else nc.vector
+            e.tensor_scalar(out=n2c[g][:], in0=n2[g][:], scalar1=TINY, scalar2=1.0, op0=ALU.max, op1=ALU.mult)
+            e.tensor_scalar(out=n2w[g][:], in0=n2[g][:], scalar1=TINY, scalar2=col(W2SQ), op0=ALU.max, op1=ALU.mult)
 
         def PW(g):
             nc.gpsimd.tensor_tensor(out=rn[g][:], in0=n2c[g][:], in1=mhalf[:], op=ALU.pow)
@@ -206,15 +207,19 @@ def tile_adaptiveattention_pa_kernel(tc, query, key, Wq, bq, Wk, bk, scoring_wei
             ew_copy(eng, rkb_sb[b][:], bc[("r", b)][:])
 
         dot = {}
-        zt = {}
         gp = {}
-        t2 = {}
-        mn = {}
-        ssum = {}
-        rs = {}
+        nsb = {}
+        zt = [keep.tile([P, 2048], F32, name="zt%d" % b) for b in range(2)]
+        t2 = [keep.tile([P, 2048], F32, name="t2_%d" % b) for b in range(2)]
+        mn = [keep.tile([P, 4], F32, name="mn%d" % b) for b in range(2)]
+        ssum = [keep.tile([P, 4], F32, name="ssum%d" % b) for b in range(2)]
+        rs = [keep.tile([P, 4], F32, name="rs%d" % b) for b in range(2)]
 
-        def D(b, n, tag="dt"):
-            a = bank("dot%d_%d" % (b, n), tag)
+        def sl(t, n0, c=1):
+            return t[:, 512 * n0 : 512 * (n0 + c)]
+
+        def D(b, n):
+            a = bank("dot%d_%d" % (b, n), "dt")
             nc.tensor.matmul_mx(out=a[:],
                                 lhsT=qk_c[2 * b + 1][:, n * 128 : n * 128 + 128].bitcast(FP8X4),
                                 lhsT_scale=qk_s[2 * b + 1][:, n * 128 : n * 128 + 128],
@@ -223,19 +228,15 @@ def tile_adaptiveattention_pa_kernel(tc, query, key, Wq, bq, Wk, bk, scoring_wei
             dot[(b, n)] = a
 
         def A(b, n):
-            z = work.tile([P, 512], F32, name="z%d_%d" % (b, n), tag="z", bufs=8)
-            nc.vector.scalar_tensor_tensor(out=z[:], in0=dot[(b, n)][:], scalar=col(M2W2), in1=kn2w_sb[b][:],
+            nc.vector.scalar_tensor_tensor(out=sl(zt[b], n), in0=dot[(b, n)][:], scalar=col(M2W2), in1=kn2w_sb[b][:],
                                            op0=ALU.mult, op1=ALU.add)
-            zt[(b, n)] = z
 
         def B(b, n):
-            z = zt[(b, n)]
-            nc.vector.tensor_scalar(out=z[:], in0=z[:], scalar1=n2w[2 * b + 1][:, n : n + 1], scalar2=TINY,
-                                    op0=ALU.add, op1=ALU.max)
+            nc.vector.tensor_scalar(out=sl(zt[b], n), in0=sl(zt[b], n), scalar1=n2w[2 * b + 1][:, n : n + 1],
+                                    scalar2=TINY, op0=ALU.add, op1=ALU.max)
 
-        def C(b, n):
-            z = zt[(b, n)]
-            nc.scalar.activation(out=z[:], in_=z[:], func=ACT.Sqrt)
+        def C(b, n0, c):
+            nc.scalar.activation(out=sl(zt[b], n0, c), in_=sl(zt[b], n0, c), func=ACT.Sqrt)
 
         def DG(b, n, eng="g"):
             g = work.tile([P, 512], F32, name="gp%d_%d" % (b, n), tag="gp", bufs=BUFS["gp"])
@@ -251,82 +252,81 @@ def tile_adaptiveattention_pa_kernel(tc, query, key, Wq, bq, Wk, bk, scoring_wei
             gp[(b, n)] = g
 
         def E(b, n):
-            t = work.tile([P, 512], F32, name="t2_%d_%d" % (b, n), tag="t2", bufs=8)
-            nc.vector.scalar_tensor_tensor(out=t[:], in0=gp[(b, n)][:], scalar=col(CC), in1=dot[(b, n)][:],
+            nc.vector.scalar_tensor_tensor(out=sl(t2[b], n), in0=gp[(b, n)][:], scalar=col(CC), in1=dot[(b, n)][:],
                                            op0=ALU.min, op1=ALU.mult)
-            t2[(b, n)] = t
 
-        def F(b, n, eng="v"):
-            t = t2[(b, n)]
-            if eng == "g":
-                nc.gpsimd.tensor_tensor(out=t[:], in0=zt[(b, n)][:], in1=t[:], op=ALU.subtract)
-            else:
-                nc.vector.tensor_tensor(out=t[:], in0=zt[(b, n)][:], in1=t[:], op=ALU.subtract)
+        def F(b, n0, c, eng="v"):
+            e = nc.gpsimd if eng == "g" else nc.vector
+            e.tensor_tensor(out=sl(t2[b], n0, c), in0=sl(zt[b], n0, c), in1=sl(t2[b], n0, c), op=ALU.subtract)
 
-        def M(b, n):
-            m = work.tile([P, 1], F32, name="mn%d_%d" % (b, n), tag="mn", bufs=8)
-            nc.vector.tensor_reduce(out=m[:], in_=t2[(b, n)][:], axis=AX.X, op=ALU.min)
-            mn[(b, n)] = m
+        def FP(b, n):
+            a = bank("nsc%d_%d" % (b, n), "dt")
+            nc.tensor.matmul(out=a[:], lhsT=ident[:], rhs=sl(zt[b], n), start=True, stop=False)
+            nc.tensor.matmul(out=a[:], lhsT=nident[:], rhs=sl(t2[b], n), start=False, stop=True)
+            nsb[(b, n)] = a
+
+        def M(b, n0, c):
+            nc.vector.tensor_reduce(out=mn[b][:, n0 : n0 + c], in_=sl(t2[b], n0, c).rearrange("p (n j) -> p n j", n=c),
+                                    axis=AX.X, op=ALU.min)
+
+        def MP(b, n):
+            nc.vector.tensor_reduce(out=mn[b][:, n : n + 1], in_=nsb[(b, n)][:], axis=AX.X, op=ALU.min)
 
         def H(b, n):
-            t = t2[(b, n)]
-            s = work.tile([P, 1], F32, name="ss%d_%d" % (b, n), tag="ss", bufs=8)
-            nc.scalar.activation(out=t[:], in_=t[:], func=ACT.Exp, bias=mn[(b, n)][:, 0:1], scale=-1.0,
-                                 accum_out=s[:])
-            ssum[(b, n)] = s
+            src = nsb[(b, n)][:] if (b, n) in nsb else sl(t2[b], n)
+            nc.scalar.activation(out=sl(t2[b], n), in_=src, func=ACT.Exp, bias=mn[b][:, n : n + 1], scale=-1.0,
+                                 accum_out=ssum[b][:, n : n + 1])
 
-        def R(b, n):
-            r = work.tile([P, 1], F32, name="rs%d_%d" % (b, n), tag="rs", bufs=8)
-            nc.vector.reciprocal(out=r[:], in_=ssum[(b, n)][:])
-            rs[(b, n)] = r
+        def R(b, n0, c):
+            nc.vector.reciprocal(out=rs[b][:, n0 : n0 + c], in_=ssum[b][:, n0 : n0 + c])
 
         def I(b, n, eng):
-            t = t2[(b, n)]
-            r = rs[(b, n)]
+            t = sl(t2[b], n)
+            r = rs[b][:, n : n + 1]
             if eng == "s":
-                nc.scalar.activation(out=t[:], in_=t[:], func=ACT.Copy, scale=r[:, 0:1])
+                nc.scalar.activation(out=t, in_=t, func=ACT.Copy, scale=r)
             elif eng == "g":
-                nc.gpsimd.tensor_scalar(out=t[:], in0=t[:], scalar1=r[:, 0:1], scalar2=0.0, op0=ALU.mult, op1=ALU.add)
+                nc.gpsimd.tensor_scalar(out=t, in0=t, scalar1=r, scalar2=0.0, op0=ALU.mult, op1=ALU.add)
             else:
-                nc.vector.tensor_scalar(out=t[:], in0=t[:], scalar1=r[:, 0:1], scalar2=None, op0=ALU.mult)
+                nc.vector.tensor_scalar(out=t, in0=t, scalar1=r, scalar2=None, op0=ALU.mult)
 
-        def ST(b, n):
-            nc.sync.dma_start(out=out[b].rearrange("(r n) j -> r n j", n=4)[:, n, :], in_=t2[(b, n)][:])
+        def ST(b, n0, c):
+            nc.sync.dma_start(out=out[b].rearrange("(r n) j -> r n j", n=4)[:, n0 : n0 + c, :],
+                              in_=sl(t2[b], n0, c).rearrange("p (n j) -> p n j", n=c))
 
         T(0); T(2); EV(0, "s"); T(3); EV(2, "s"); T(1)
-        EV(3, "s"); QZ(2); T(4); EXPW(); EV(1, "s"); QZ(3)
-        T(6); EV(4, "s"); QZ(1); T(7); QZ(0); EV(6, "s")
-        QZ(4); T(5); WC(); EV(7, "s"); QZ(6); PJ(0, 3)
-        EV(5, "s"); QZ(7); PJ(0, 1); PJ(0, 2); TH(0, 3); QZ(5)
-        PJ(0, 0); T(9); TH(0, 2); T(8); TH(0, 1); EV(9, "v")
-        PJ(1, 2); TH(0, 0); PJ(1, 0); QZ(9); PJ(1, 3); TH(1, 2)
-        EV(8, "v"); PJ(1, 1); T(11); TH(1, 0); QZ(8); TH(1, 3)
-        T(10); EV(11, "v"); TH(1, 1); PJ(2, 2); EV(10, "v"); PJ(2, 0)
-        TH(2, 2); PJ(2, 1); PJ(2, 3); QZ(10); TH(2, 1); TQ(0, 0)
-        RG(1); TH(2, 0); TQ(0, 3); SQ(0, 0); TQ(0, 2); QZ(11)
-        RG(0); SQ(0, 3); TQ(0, 1); SQ(0, 2); PJ(3, 3); PJ(3, 2)
-        QG(1); TH(2, 3); PJ(3, 0); QG(0); SQ(0, 1); PJ(3, 1)
-        TQ(1, 3); RG(2); TH(3, 2); TQ(1, 2); TH(3, 0); TQ(1, 0)
-        NC(0); TH(3, 3); QG(2); PW(0); TQ(1, 1); TH(3, 1)
-        BK(0); SQ(1, 3); RG(3); TQ(2, 2); SQ(1, 2); D(0, 3)
-        SQ(1, 0); QG(3); D(0, 0); BR(0); SQ(1, 1); D(0, 1)
-        CK(0, "s"); NC(1); D(0, 2); TQ(2, 0); PW(1); SQ(2, 2)
-        A(0, 3); TQ(3, 1); CR(0, "s"); A(0, 0); TQ(2, 3); B(0, 3)
-        DG(0, 3, "g"); B(0, 0); C(0, 3); A(0, 1); A(0, 2); DG(0, 0, "g")
-        B(0, 1); E(0, 3); DG(0, 1, "g"); E(0, 0); TQ(2, 1); C(0, 0)
-        DG(0, 2, "g"); F(0, 3, "v"); TQ(3, 0); SQ(2, 0); E(0, 1); D(1, 1)
-        SQ(2, 1); B(0, 2); TQ(3, 2); SQ(2, 3); E(0, 2); C(0, 2)
-        F(0, 0, "v"); TQ(3, 3); SQ(3, 1); NC(2); F(0, 2, "v"); PW(2)
-        BK(1); SQ(3, 0); M(0, 0); D(1, 2); SQ(3, 2); D(1, 3)
-        M(0, 2); D(1, 0); CK(1, "s"); BR(1); M(0, 3); SQ(3, 3)
-        A(1, 2); C(0, 1); NC(3); A(1, 3); CR(1, "s"); PW(3)
-        A(1, 1); B(1, 2); F(0, 1, "v"); DG(1, 2, "g"); B(1, 1); A(1, 0)
-        C(1, 1); DG(1, 0, "g"); B(1, 3); C(1, 2); E(1, 2); C(1, 3)
-        DG(1, 1, "g"); B(1, 0); M(0, 1); C(1, 0); DG(1, 3, "g"); F(1, 2, "v")
-        H(0, 0); E(1, 0); E(1, 3); E(1, 1); M(1, 2); H(0, 1)
-        F(1, 0, "v"); H(0, 3); F(1, 1, "v"); H(1, 2); M(1, 0); H(0, 2)
-        R(0, 3); R(0, 1); R(0, 0); F(1, 3, "v"); H(1, 0); R(1, 2)
-        I(0, 0, "v"); I(0, 1, "v"); ST(0, 0); I(1, 2, "v"); R(1, 0); M(1, 1)
-        ST(1, 2); ST(0, 1); I(1, 0, "v"); H(1, 1); M(1, 3); ST(1, 0)
-        I(0, 3, "v"); H(1, 3); R(0, 2); R(1, 1); ST(0, 3); I(0, 2, "v")
-        I(1, 1, "v"); ST(0, 2); R(1, 3); ST(1, 1); I(1, 3, "v"); ST(1, 3)
+        EV(3, "s"); T(4); EV(1, "s"); QZ(1); T(6); EV(4, "s")
+        QZ(0); T(7); EV(6, "s"); T(5); EXPW(); EV(7, "v")
+        PJ(0, 2); EV(5, "s"); QZ(3); PJ(0, 0); PJ(0, 3); TH(0, 2)
+        QZ(2); PJ(0, 1); T(9); TH(0, 0); T(8); TH(0, 3)
+        EV(9, "v"); PJ(1, 3); TH(0, 1); EV(8, "v"); PJ(1, 0); TH(1, 3)
+        PJ(1, 2); QZ(4); PJ(1, 1); TH(1, 2); PJ(2, 3); TH(1, 0)
+        PJ(2, 2); PJ(2, 1); TH(2, 3); TQ(0, 1); TH(1, 1); T(10)
+        TH(2, 2); RG(1); TQ(1, 3); TH(2, 1); TQ(0, 0); SQ(0, 1)
+        RG(0); T(11); SQ(0, 0); TQ(1, 2); SQ(1, 3); WC()
+        TQ(0, 3); EV(10, "v"); SQ(1, 2); TQ(0, 2); EV(11, "v"); SQ(0, 3)
+        TQ(1, 0); QZ(5); SQ(0, 2); TQ(1, 1); QG(1); SQ(1, 0)
+        NC(0, "g"); PJ(2, 0); QG(0); SQ(1, 1); PJ(3, 2); PW(0)
+        PJ(3, 0); TH(2, 0); PJ(3, 1); PJ(3, 3); TH(3, 2); BK(0)
+        RG(2); NC(1, "g"); TH(3, 1); BR(0); PW(1); TH(3, 0)
+        TQ(2, 0); QG(2); TH(3, 3); TQ(2, 2); CK(0, "s"); RG(3)
+        TQ(2, 1); CR(0, "s"); D(0, 3); D(0, 0); SQ(2, 0); A(0, 3)
+        DG(0, 3, "g"); D(0, 2); TQ(2, 3); SQ(2, 1); QG(3); TQ(3, 1)
+        DG(0, 0, "g"); SQ(2, 2); A(0, 2); TQ(3, 2); SQ(2, 3); A(0, 0)
+        DG(0, 2, "g"); SQ(3, 1); TQ(3, 3); E(0, 3); SQ(3, 2); TQ(3, 0)
+        B(0, 3); NC(2, "g"); E(0, 0); SQ(3, 3); E(0, 2); DG(0, 1, "g")
+        BK(1); SQ(3, 0); B(0, 0); D(0, 1); CK(1, "s"); B(0, 2)
+        D(1, 0); PW(2); A(0, 1); D(1, 2); C(0, 0, 1); D(1, 3)
+        A(1, 0); NC(3, "g"); E(0, 1); BR(1); B(0, 1); PW(3)
+        D(1, 1); A(1, 3); A(1, 2); CR(1, "s"); FP(0, 0); A(1, 1)
+        C(0, 1, 1); DG(1, 2, "g"); B(1, 2); C(0, 2, 1); B(1, 1); B(1, 0)
+        C(0, 3, 1); DG(1, 3, "g"); B(1, 3); E(1, 2); C(1, 2, 1); FP(0, 2)
+        MP(0, 0); DG(1, 0, "g"); C(1, 3, 1); F(1, 2, 1, "v"); C(1, 0, 1); DG(1, 1, "g")
+        E(1, 3); C(1, 1, 1); E(1, 0); H(0, 0); FP(0, 1); F(1, 3, 1, "v")
+        MP(0, 2); M(1, 3, 1); F(1, 0, 1, "v"); H(0, 2); FP(0, 3); R(0, 0, 1)
+        MP(0, 1); I(0, 0, "g"); R(0, 2, 1); E(1, 1); H(0, 1); I(0, 2, "g")
+        M(1, 0, 1); H(1, 3); R(0, 1, 1); F(1, 1, 1, "v"); H(1, 0); I(0, 1, "g")
+        ST(0, 2, 1); ST(0, 0, 1); M(1, 2, 1); R(1, 3, 1); M(1, 1, 1); H(1, 2)
+        ST(0, 1, 1); MP(0, 3); H(1, 1); I(1, 3, "v"); H(0, 3); R(1, 2, 1)
+        R(1, 0, 1); ST(1, 3, 1); I(1, 2, "v"); I(1, 0, "g"); R(1, 1, 1); ST(1, 2, 1)
+        I(1, 1, "v"); R(0, 3, 1); ST(1, 1, 1); I(0, 3, "g"); ST(1, 0, 1); ST(0, 3, 1)

@@ -16,7 +16,7 @@ AX = mybir.AxisListType
 
 P = 128
 TINY = 1e-30
-BUFS = {"f":3,"gq":2,"gp":8,"junk":2}
+BUFS = {"tp":2,"tq":2,"pj":2,"dt":2,"f":3,"gq":2,"gp":8,"junk":2}
 
 
 def tile_adaptiveattention_pa_kernel(tc, query, key, Wq, bq, Wk, bk, scoring_weights, out):
@@ -62,8 +62,6 @@ def tile_adaptiveattention_pa_kernel(tc, query, key, Wq, bq, Wk, bk, scoring_wei
 
         ident = keep.tile([P, P], F32, name="ident")
         make_identity(nc, ident[:])
-        nident = keep.tile([P, P], F32, name="nident")
-        nc.gpsimd.tensor_scalar(out=nident[:], in0=ident[:], scalar1=-1.0, scalar2=0.0, op0=ALU.mult, op1=ALU.add)
         mhalf = keep.tile([P, 4], F32, name="mhalf")
         nc.vector.memset(mhalf[:], -0.5)
 
@@ -114,14 +112,15 @@ def tile_adaptiveattention_pa_kernel(tc, query, key, Wq, bq, Wk, bk, scoring_wei
             xt[i] = t
 
         def EV(i, eng):
-            o, h = i // 2, i % 2
-            if o not in grp:
-                grp[o] = keep.tile([P, 2048], BF16, name="grp%d" % o, align_bytes=64)
-            ew_copy(eng, grp[o][:, 1024 * h : 1024 * h + 1024].bitcast(F32).rearrange("p (r u) -> p r u", u=2),
+            g = keep.tile([P, 1024], BF16, name="grp%d" % i, align_bytes=64)
+            ew_copy(eng, g[:].bitcast(F32).rearrange("p (r u) -> p r u", u=2),
                     xt[i][:].rearrange("p (u r) -> p r u", u=2))
+            grp[i] = g
 
-        def QZ(o):
-            nc.vector.quantize_mx(out=in_c[o][:].bitcast(FP8X4), scales=in_s[o][:], in_=grp[o][:])
+        def QZ(i):
+            o, h = i // 2, i % 2
+            nc.vector.quantize_mx(out=in_c[o][:, 256 * h : 256 * h + 256].bitcast(FP8X4),
+                                  scales=in_s[o][:, 256 * h : 256 * h + 256], in_=grp[i][:])
 
         g_w = [0, 2, 0, 2]
         g_x = [1, 3, 4, 5]
@@ -173,10 +172,10 @@ def tile_adaptiveattention_pa_kernel(tc, query, key, Wq, bq, Wk, bk, scoring_wei
             j = work.tile([P, 512], BF16, name="jk%d_%d" % (g, n), tag="junk", bufs=BUFS["junk"])
             nc.scalar.activation(out=j[:], in_=tq[(g, n)][:], func=ACT.Square, accum_out=n2[g][:, n : n + 1])
 
-        def NC(g, eng):
-            e = nc.gpsimd if eng == "g" else nc.vector
-            e.tensor_scalar(out=n2c[g][:], in0=n2[g][:], scalar1=TINY, scalar2=1.0, op0=ALU.max, op1=ALU.mult)
-            e.tensor_scalar(out=n2w[g][:], in0=n2[g][:], scalar1=TINY, scalar2=col(W2SQ), op0=ALU.max, op1=ALU.mult)
+        def NC(g):
+            nc.vector.tensor_scalar(out=n2c[g][:], in0=n2[g][:], scalar1=TINY, scalar2=None, op0=ALU.max)
+            nc.vector.tensor_scalar(out=n2w[g][:], in0=n2[g][:], scalar1=TINY, scalar2=col(W2SQ),
+                                    op0=ALU.max, op1=ALU.mult)
 
         def PW(g):
             nc.gpsimd.tensor_tensor(out=rn[g][:], in0=n2c[g][:], in1=mhalf[:], op=ALU.pow)
@@ -207,19 +206,15 @@ def tile_adaptiveattention_pa_kernel(tc, query, key, Wq, bq, Wk, bk, scoring_wei
             ew_copy(eng, rkb_sb[b][:], bc[("r", b)][:])
 
         dot = {}
+        zt = {}
         gp = {}
-        nsb = {}
-        zt = [keep.tile([P, 2048], F32, name="zt%d" % b) for b in range(2)]
-        t2 = [keep.tile([P, 2048], F32, name="t2_%d" % b) for b in range(2)]
-        mn = [keep.tile([P, 4], F32, name="mn%d" % b) for b in range(2)]
-        ssum = [keep.tile([P, 4], F32, name="ssum%d" % b) for b in range(2)]
-        rs = [keep.tile([P, 4], F32, name="rs%d" % b) for b in range(2)]
+        t2 = {}
+        mn = {}
+        ssum = {}
+        rs = {}
 
-        def sl(t, n0, c=1):
-            return t[:, 512 * n0 : 512 * (n0 + c)]
-
-        def D(b, n):
-            a = bank("dot%d_%d" % (b, n), "dt")
+        def D(b, n, tag="dt"):
+            a = bank("dot%d_%d" % (b, n), tag)
             nc.tensor.matmul_mx(out=a[:],
                                 lhsT=qk_c[2 * b + 1][:, n * 128 : n * 128 + 128].bitcast(FP8X4),
                                 lhsT_scale=qk_s[2 * b + 1][:, n * 128 : n * 128 + 128],
@@ -228,15 +223,19 @@ def tile_adaptiveattention_pa_kernel(tc, query, key, Wq, bq, Wk, bk, scoring_wei
             dot[(b, n)] = a
 
         def A(b, n):
-            nc.vector.scalar_tensor_tensor(out=sl(zt[b], n), in0=dot[(b, n)][:], scalar=col(M2W2), in1=kn2w_sb[b][:],
+            z = work.tile([P, 512], F32, name="z%d_%d" % (b, n), tag="z", bufs=8)
+            nc.vector.scalar_tensor_tensor(out=z[:], in0=dot[(b, n)][:], scalar=col(M2W2), in1=kn2w_sb[b][:],
                                            op0=ALU.mult, op1=ALU.add)
+            zt[(b, n)] = z
 
         def B(b, n):
-            nc.vector.tensor_scalar(out=sl(zt[b], n), in0=sl(zt[b], n), scalar1=n2w[2 * b + 1][:, n : n + 1],
-                                    scalar2=TINY, op0=ALU.add, op1=ALU.max)
+            z = zt[(b, n)]
+            nc.vector.tensor_scalar(out=z[:], in0=z[:], scalar1=n2w[2 * b + 1][:, n : n + 1], scalar2=TINY,
+                                    op0=ALU.add, op1=ALU.max)
 
-        def C(b, n0, c):
-            nc.scalar.activation(out=sl(zt[b], n0, c), in_=sl(zt[b], n0, c), func=ACT.Sqrt)
+        def C(b, n):
+            z = zt[(b, n)]
+            nc.scalar.activation(out=z[:], in_=z[:], func=ACT.Sqrt)
 
         def DG(b, n, eng="g"):
             g = work.tile([P, 512], F32, name="gp%d_%d" % (b, n), tag="gp", bufs=BUFS["gp"])
@@ -252,81 +251,82 @@ def tile_adaptiveattention_pa_kernel(tc, query, key, Wq, bq, Wk, bk, scoring_wei
             gp[(b, n)] = g
 
         def E(b, n):
-            nc.vector.scalar_tensor_tensor(out=sl(t2[b], n), in0=gp[(b, n)][:], scalar=col(CC), in1=dot[(b, n)][:],
+            t = work.tile([P, 512], F32, name="t2_%d_%d" % (b, n), tag="t2", bufs=8)
+            nc.vector.scalar_tensor_tensor(out=t[:], in0=gp[(b, n)][:], scalar=col(CC), in1=dot[(b, n)][:],
                                            op0=ALU.min, op1=ALU.mult)
+            t2[(b, n)] = t
 
-        def F(b, n0, c, eng="v"):
-            e = nc.gpsimd if eng == "g" else nc.vector
-            e.tensor_tensor(out=sl(t2[b], n0, c), in0=sl(zt[b], n0, c), in1=sl(t2[b], n0, c), op=ALU.subtract)
+        def F(b, n, eng="v"):
+            t = t2[(b, n)]
+            if eng == "g":
+                nc.gpsimd.tensor_tensor(out=t[:], in0=zt[(b, n)][:], in1=t[:], op=ALU.subtract)
+            else:
+                nc.vector.tensor_tensor(out=t[:], in0=zt[(b, n)][:], in1=t[:], op=ALU.subtract)
 
-        def FP(b, n):
-            a = bank("nsc%d_%d" % (b, n), "dt")
-            nc.tensor.matmul(out=a[:], lhsT=ident[:], rhs=sl(zt[b], n), start=True, stop=False)
-            nc.tensor.matmul(out=a[:], lhsT=nident[:], rhs=sl(t2[b], n), start=False, stop=True)
-            nsb[(b, n)] = a
-
-        def M(b, n0, c):
-            nc.vector.tensor_reduce(out=mn[b][:, n0 : n0 + c], in_=sl(t2[b], n0, c).rearrange("p (n j) -> p n j", n=c),
-                                    axis=AX.X, op=ALU.min)
-
-        def MP(b, n):
-            nc.vector.tensor_reduce(out=mn[b][:, n : n + 1], in_=nsb[(b, n)][:], axis=AX.X, op=ALU.min)
+        def M(b, n):
+            m = work.tile([P, 1], F32, name="mn%d_%d" % (b, n), tag="mn", bufs=8)
+            nc.vector.tensor_reduce(out=m[:], in_=t2[(b, n)][:], axis=AX.X, op=ALU.min)
+            mn[(b, n)] = m
 
         def H(b, n):
-            src = nsb[(b, n)][:] if (b, n) in nsb else sl(t2[b], n)
-            nc.scalar.activation(out=sl(t2[b], n), in_=src, func=ACT.Exp, bias=mn[b][:, n : n + 1], scale=-1.0,
-                                 accum_out=ssum[b][:, n : n + 1])
+            t = t2[(b, n)]
+            s = work.tile([P, 1], F32, name="ss%d_%d" % (b, n), tag="ss", bufs=8)
+            nc.scalar.activation(out=t[:], in_=t[:], func=ACT.Exp, bias=mn[(b, n)][:, 0:1], scale=-1.0,
+                                 accum_out=s[:])
+            ssum[(b, n)] = s
 
-        def R(b, n0, c):
-            nc.vector.reciprocal(out=rs[b][:, n0 : n0 + c], in_=ssum[b][:, n0 : n0 + c])
+        def R(b, n):
+            r = work.tile([P, 1], F32, name="rs%d_%d" % (b, n), tag="rs", bufs=8)
+            nc.vector.reciprocal(out=r[:], in_=ssum[(b, n)][:])
+            rs[(b, n)] = r
 
         def I(b, n, eng):
-            t = sl(t2[b], n)
-            r = rs[b][:, n : n + 1]
+            t = t2[(b, n)]
+            r = rs[(b, n)]
             if eng == "s":
-                nc.scalar.activation(out=t, in_=t, func=ACT.Copy, scale=r)
+                nc.scalar.activation(out=t[:], in_=t[:], func=ACT.Copy, scale=r[:, 0:1])
             elif eng == "g":
-                nc.gpsimd.tensor_scalar(out=t, in0=t, scalar1=r, scalar2=0.0, op0=ALU.mult, op1=ALU.add)
+                nc.gpsimd.tensor_scalar(out=t[:], in0=t[:], scalar1=r[:, 0:1], scalar2=0.0, op0=ALU.mult, op1=ALU.add)
             else:
-                nc.vector.tensor_scalar(out=t, in0=t, scalar1=r, scalar2=None, op0=ALU.mult)
+                nc.vector.tensor_scalar(out=t[:], in0=t[:], scalar1=r[:, 0:1], scalar2=None, op0=ALU.mult)
 
-        def ST(b, n0, c):
-            nc.sync.dma_start(out=out[b].rearrange("(r n) j -> r n j", n=4)[:, n0 : n0 + c, :],
-                              in_=sl(t2[b], n0, c).rearrange("p (n j) -> p n j", n=c))
+        def ST(b, n):
+            nc.sync.dma_start(out=out[b].rearrange("(r n) j -> r n j", n=4)[:, n, :], in_=t2[(b, n)][:])
 
         T(0); T(2); EV(0, "s"); T(3); EV(2, "s"); T(1)
-        EV(3, "s"); T(4); EV(1, "s"); QZ(1); T(6); EV(4, "s")
-        QZ(0); T(7); EV(6, "s"); T(5); EXPW(); EV(7, "v")
-        PJ(0, 2); EV(5, "s"); QZ(3); PJ(0, 0); PJ(0, 3); TH(0, 2)
-        QZ(2); PJ(0, 1); T(9); TH(0, 0); T(8); TH(0, 3)
-        EV(9, "v"); PJ(1, 3); TH(0, 1); EV(8, "v"); PJ(1, 0); TH(1, 3)
-        PJ(1, 2); QZ(4); PJ(1, 1); TH(1, 2); PJ(2, 3); TH(1, 0)
-        PJ(2, 2); PJ(2, 1); TH(2, 3); TQ(0, 1); TH(1, 1); T(10)
-        TH(2, 2); RG(1); TQ(1, 3); TH(2, 1); TQ(0, 0); SQ(0, 1)
-        RG(0); T(11); SQ(0, 0); TQ(1, 2); SQ(1, 3); WC()
-        TQ(0, 3); EV(10, "v"); SQ(1, 2); TQ(0, 2); EV(11, "v"); SQ(0, 3)
-        TQ(1, 0); QZ(5); SQ(0, 2); TQ(1, 1); QG(1); SQ(1, 0)
-        NC(0, "g"); PJ(2, 0); QG(0); SQ(1, 1); PJ(3, 2); PW(0)
-        PJ(3, 0); TH(2, 0); PJ(3, 1); PJ(3, 3); TH(3, 2); BK(0)
-        RG(2); NC(1, "g"); TH(3, 1); BR(0); PW(1); TH(3, 0)
-        TQ(2, 0); QG(2); TH(3, 3); TQ(2, 2); CK(0, "s"); RG(3)
-        TQ(2, 1); CR(0, "s"); D(0, 3); D(0, 0); SQ(2, 0); A(0, 3)
-        DG(0, 3, "g"); D(0, 2); TQ(2, 3); SQ(2, 1); QG(3); TQ(3, 1)
-        DG(0, 0, "g"); SQ(2, 2); A(0, 2); TQ(3, 2); SQ(2, 3); A(0, 0)
-        DG(0, 2, "g"); SQ(3, 1); TQ(3, 3); E(0, 3); SQ(3, 2); TQ(3, 0)
-        B(0, 3); NC(2, "g"); E(0, 0); SQ(3, 3); E(0, 2); DG(0, 1, "g")
-        BK(1); SQ(3, 0); B(0, 0); D(0, 1); CK(1, "s"); B(0, 2)
-        D(1, 0); PW(2); A(0, 1); D(1, 2); C(0, 0, 1); D(1, 3)
-        A(1, 0); NC(3, "g"); E(0, 1); BR(1); B(0, 1); PW(3)
-        D(1, 1); A(1, 3); A(1, 2); CR(1, "s"); FP(0, 0); A(1, 1)
-        C(0, 1, 1); DG(1, 2, "g"); B(1, 2); C(0, 2, 1); B(1, 1); B(1, 0)
-        C(0, 3, 1); DG(1, 3, "g"); B(1, 3); E(1, 2); C(1, 2, 1); FP(0, 2)
-        MP(0, 0); DG(1, 0, "g"); C(1, 3, 1); F(1, 2, 1, "v"); C(1, 0, 1); DG(1, 1, "g")
-        E(1, 3); C(1, 1, 1); E(1, 0); H(0, 0); FP(0, 1); F(1, 3, 1, "v")
-        MP(0, 2); M(1, 3, 1); F(1, 0, 1, "v"); H(0, 2); FP(0, 3); R(0, 0, 1)
-        MP(0, 1); I(0, 0, "g"); R(0, 2, 1); E(1, 1); H(0, 1); I(0, 2, "g")
-        M(1, 0, 1); H(1, 3); R(0, 1, 1); F(1, 1, 1, "v"); H(1, 0); I(0, 1, "g")
-        ST(0, 2, 1); ST(0, 0, 1); M(1, 2, 1); R(1, 3, 1); M(1, 1, 1); H(1, 2)
-        ST(0, 1, 1); MP(0, 3); H(1, 1); I(1, 3, "v"); H(0, 3); R(1, 2, 1)
-        R(1, 0, 1); ST(1, 3, 1); I(1, 2, "v"); I(1, 0, "g"); R(1, 1, 1); ST(1, 2, 1)
-        I(1, 1, "v"); R(0, 3, 1); ST(1, 1, 1); I(0, 3, "g"); ST(1, 0, 1); ST(0, 3, 1)
+        EV(3, "s"); QZ(2); T(4); EXPW(); EV(1, "s"); QZ(3)
+        T(6); EV(4, "s"); QZ(1); T(7); QZ(0); EV(6, "s")
+        QZ(4); T(5); WC(); EV(7, "s"); QZ(6); PJ(0, 3)
+        EV(5, "s"); QZ(7); PJ(0, 1); PJ(0, 2); TH(0, 3); QZ(5)
+        PJ(0, 0); T(9); TH(0, 2); T(8); TH(0, 1); EV(9, "v")
+        PJ(1, 2); TH(0, 0); PJ(1, 0); QZ(9); PJ(1, 3); TH(1, 2)
+        EV(8, "v"); PJ(1, 1); T(11); TH(1, 0); QZ(8); TH(1, 3)
+        T(10); EV(11, "v"); TH(1, 1); PJ(2, 2); EV(10, "v"); PJ(2, 0)
+        TH(2, 2); PJ(2, 1); PJ(2, 3); QZ(10); TH(2, 1); TQ(0, 0)
+        RG(1); TH(2, 0); TQ(0, 3); SQ(0, 0); TQ(0, 2); QZ(11)
+        RG(0); SQ(0, 3); TQ(0, 1); SQ(0, 2); PJ(3, 3); PJ(3, 2)
+        QG(1); TH(2, 3); PJ(3, 0); QG(0); SQ(0, 1); PJ(3, 1)
+        TQ(1, 3); RG(2); TH(3, 2); TQ(1, 2); TH(3, 0); TQ(1, 0)
+        NC(0); TH(3, 3); QG(2); PW(0); TQ(1, 1); TH(3, 1)
+        BK(0); SQ(1, 3); RG(3); TQ(2, 2); SQ(1, 2); D(0, 3)
+        SQ(1, 0); QG(3); D(0, 0); BR(0); SQ(1, 1); D(0, 1)
+        CK(0, "s"); NC(1); D(0, 2); TQ(2, 0); PW(1); SQ(2, 2)
+        A(0, 3); TQ(3, 1); CR(0, "s"); A(0, 0); TQ(2, 3); B(0, 3)
+        DG(0, 3, "v"); B(0, 0); C(0, 3); A(0, 1); A(0, 2); DG(0, 0, "v")
+        B(0, 1); E(0, 3); DG(0, 1, "v"); E(0, 0); TQ(2, 1); C(0, 0)
+        DG(0, 2, "v"); F(0, 3, "v"); TQ(3, 0); SQ(2, 0); E(0, 1); D(1, 1)
+        SQ(2, 1); B(0, 2); TQ(3, 2); SQ(2, 3); E(0, 2); C(0, 2)
+        F(0, 0, "v"); TQ(3, 3); SQ(3, 1); NC(2); F(0, 2, "v"); PW(2)
+        BK(1); SQ(3, 0); M(0, 0); D(1, 2); SQ(3, 2); D(1, 3)
+        M(0, 2); D(1, 0); CK(1, "s"); BR(1); M(0, 3); SQ(3, 3)
+        A(1, 2); C(0, 1); NC(3); A(1, 3); CR(1, "s"); PW(3)
+        A(1, 1); B(1, 2); F(0, 1, "v"); DG(1, 2, "v"); B(1, 1); A(1, 0)
+        C(1, 1); DG(1, 0, "v"); B(1, 3); C(1, 2); E(1, 2); C(1, 3)
+        DG(1, 1, "v"); B(1, 0); M(0, 1); C(1, 0); DG(1, 3, "v"); F(1, 2, "v")
+        H(0, 0); E(1, 0); E(1, 3); E(1, 1); M(1, 2); H(0, 1)
+        F(1, 0, "v"); H(0, 3); F(1, 1, "v"); H(1, 2); M(1, 0); H(0, 2)
+        R(0, 3); R(0, 1); R(0, 0); F(1, 3, "v"); H(1, 0); R(1, 2)
+        I(0, 0, "v"); I(0, 1, "v"); ST(0, 0); I(1, 2, "v"); R(1, 0); M(1, 1)
+        ST(1, 2); ST(0, 1); I(1, 0, "v"); H(1, 1); M(1, 3); ST(1, 0)
+        I(0, 3, "v"); H(1, 3); R(0, 2); R(1, 1); ST(0, 3); I(0, 2, "v")
+        I(1, 1, "v"); ST(0, 2); R(1, 3); ST(1, 1); I(1, 3, "v"); ST(1, 3)

@@ -16,7 +16,7 @@ AX = mybir.AxisListType
 
 P = 128
 TINY = 1e-30
-BUFS = {"tp":2,"tq":2,"pj":2,"dt":2,"f":3,"gq":2,"gp":8,"junk":2}
+BUFS = {"f":3,"gq":2,"gp":8,"junk":2}
 
 
 def tile_adaptiveattention_pa_kernel(tc, query, key, Wq, bq, Wk, bk, scoring_weights, out):
@@ -112,15 +112,20 @@ def tile_adaptiveattention_pa_kernel(tc, query, key, Wq, bq, Wk, bk, scoring_wei
             xt[i] = t
 
         def EV(i, eng):
-            g = keep.tile([P, 1024], BF16, name="grp%d" % i, align_bytes=64)
-            ew_copy(eng, g[:].bitcast(F32).rearrange("p (r u) -> p r u", u=2),
+            o, h = i // 2, i % 2
+            if o not in grp:
+                grp[o] = keep.tile([P, 2048], BF16, name="grp%d" % o, align_bytes=64)
+            ew_copy(eng, grp[o][:, 1024 * h : 1024 * h + 1024].bitcast(F32).rearrange("p (r u) -> p r u", u=2),
                     xt[i][:].rearrange("p (u r) -> p r u", u=2))
-            grp[i] = g
 
-        def QZ(i):
+        def QH(i):
             o, h = i // 2, i % 2
             nc.vector.quantize_mx(out=in_c[o][:, 256 * h : 256 * h + 256].bitcast(FP8X4),
-                                  scales=in_s[o][:, 256 * h : 256 * h + 256], in_=grp[i][:])
+                                  scales=in_s[o][:, 256 * h : 256 * h + 256],
+                                  in_=grp[o][:, 1024 * h : 1024 * h + 1024])
+
+        def QZ(o):
+            nc.vector.quantize_mx(out=in_c[o][:].bitcast(FP8X4), scales=in_s[o][:], in_=grp[o][:])
 
         g_w = [0, 2, 0, 2]
         g_x = [1, 3, 4, 5]
@@ -172,10 +177,10 @@ def tile_adaptiveattention_pa_kernel(tc, query, key, Wq, bq, Wk, bk, scoring_wei
             j = work.tile([P, 512], BF16, name="jk%d_%d" % (g, n), tag="junk", bufs=BUFS["junk"])
             nc.scalar.activation(out=j[:], in_=tq[(g, n)][:], func=ACT.Square, accum_out=n2[g][:, n : n + 1])
 
-        def NC(g):
-            nc.vector.tensor_scalar(out=n2c[g][:], in0=n2[g][:], scalar1=TINY, scalar2=None, op0=ALU.max)
-            nc.vector.tensor_scalar(out=n2w[g][:], in0=n2[g][:], scalar1=TINY, scalar2=col(W2SQ),
-                                    op0=ALU.max, op1=ALU.mult)
+        def NC(g, eng):
+            e = nc.gpsimd if eng == "g" else nc.vector
+            e.tensor_scalar(out=n2c[g][:], in0=n2[g][:], scalar1=TINY, scalar2=1.0, op0=ALU.max, op1=ALU.mult)
+            e.tensor_scalar(out=n2w[g][:], in0=n2[g][:], scalar1=TINY, scalar2=col(W2SQ), op0=ALU.max, op1=ALU.mult)
 
         def PW(g):
             nc.gpsimd.tensor_tensor(out=rn[g][:], in0=n2c[g][:], in1=mhalf[:], op=ALU.pow)
@@ -206,15 +211,18 @@ def tile_adaptiveattention_pa_kernel(tc, query, key, Wq, bq, Wk, bk, scoring_wei
             ew_copy(eng, rkb_sb[b][:], bc[("r", b)][:])
 
         dot = {}
-        zt = {}
         gp = {}
-        t2 = {}
-        mn = {}
-        ssum = {}
-        rs = {}
+        zt = [keep.tile([P, 2048], F32, name="zt%d" % b) for b in range(2)]
+        t2 = [keep.tile([P, 2048], F32, name="t2_%d" % b) for b in range(2)]
+        mn = [keep.tile([P, 4], F32, name="mn%d" % b) for b in range(2)]
+        ssum = [keep.tile([P, 4], F32, name="ssum%d" % b) for b in range(2)]
+        rs = [keep.tile([P, 4], F32, name="rs%d" % b) for b in range(2)]
 
-        def D(b, n, tag="dt"):
-            a = bank("dot%d_%d" % (b, n), tag)
+        def sl(t, n0, c=1):
+            return t[:, 512 * n0 : 512 * (n0 + c)]
+
+        def D(b, n):
+            a = bank("dot%d_%d" % (b, n), "dt")
             nc.tensor.matmul_mx(out=a[:],
                                 lhsT=qk_c[2 * b + 1][:, n * 128 : n * 128 + 128].bitcast(FP8X4),
                                 lhsT_scale=qk_s[2 * b + 1][:, n * 128 : n * 128 + 128],
@@ -223,19 +231,15 @@ def tile_adaptiveattention_pa_kernel(tc, query, key, Wq, bq, Wk, bk, scoring_wei
             dot[(b, n)] = a
 
         def A(b, n):
-            z = work.tile([P, 512], F32, name="z%d_%d" % (b, n), tag="z", bufs=8)
-            nc.vector.scalar_tensor_tensor(out=z[:], in0=dot[(b, n)][:], scalar=col(M2W2), in1=kn2w_sb[b][:],
+            nc.vector.scalar_tensor_tensor(out=sl(zt[b], n), in0=dot[(b, n)][:], scalar=col(M2W2), in1=kn2w_sb[b][:],
                                            op0=ALU.mult, op1=ALU.add)
-            zt[(b, n)] = z
 
         def B(b, n):
-            z = zt[(b, n)]
-            nc.vector.tensor_scalar(out=z[:], in0=z[:], scalar1=n2w[2 * b + 1][:, n : n + 1], scalar2=TINY,
-                                    op0=ALU.add, op1=ALU.max)
+            nc.vector.tensor_scalar(out=sl(zt[b], n), in0=sl(zt[b], n), scalar1=n2w[2 * b + 1][:, n : n + 1],
+                                    scalar2=TINY, op0=ALU.add, op1=ALU.max)
 
-        def C(b, n):
-            z = zt[(b, n)]
-            nc.scalar.activation(out=z[:], in_=z[:], func=ACT.Sqrt)
+        def C(b, n0, c):
+            nc.scalar.activation(out=sl(zt[b], n0, c), in_=sl(zt[b], n0, c), func=ACT.Sqrt)
 
         def DG(b, n, eng="g"):
             g = work.tile([P, 512], F32, name="gp%d_%d" % (b, n), tag="gp", bufs=BUFS["gp"])
@@ -251,82 +255,72 @@ def tile_adaptiveattention_pa_kernel(tc, query, key, Wq, bq, Wk, bk, scoring_wei
             gp[(b, n)] = g
 
         def E(b, n):
-            t = work.tile([P, 512], F32, name="t2_%d_%d" % (b, n), tag="t2", bufs=8)
-            nc.vector.scalar_tensor_tensor(out=t[:], in0=gp[(b, n)][:], scalar=col(CC), in1=dot[(b, n)][:],
+            nc.vector.scalar_tensor_tensor(out=sl(t2[b], n), in0=gp[(b, n)][:], scalar=col(CC), in1=dot[(b, n)][:],
                                            op0=ALU.min, op1=ALU.mult)
-            t2[(b, n)] = t
 
-        def F(b, n, eng="v"):
-            t = t2[(b, n)]
-            if eng == "g":
-                nc.gpsimd.tensor_tensor(out=t[:], in0=zt[(b, n)][:], in1=t[:], op=ALU.subtract)
-            else:
-                nc.vector.tensor_tensor(out=t[:], in0=zt[(b, n)][:], in1=t[:], op=ALU.subtract)
+        def F(b, n0, c, eng="v"):
+            e = nc.gpsimd if eng == "g" else nc.vector
+            e.tensor_tensor(out=sl(t2[b], n0, c), in0=sl(zt[b], n0, c), in1=sl(t2[b], n0, c), op=ALU.subtract)
 
-        def M(b, n):
-            m = work.tile([P, 1], F32, name="mn%d_%d" % (b, n), tag="mn", bufs=8)
-            nc.vector.tensor_reduce(out=m[:], in_=t2[(b, n)][:], axis=AX.X, op=ALU.min)
-            mn[(b, n)] = m
+        def M(b, n0, c):
+            nc.vector.tensor_reduce(out=mn[b][:, n0 : n0 + c], in_=sl(t2[b], n0, c).rearrange("p (n j) -> p n j", n=c),
+                                    axis=AX.X, op=ALU.min)
 
         def H(b, n):
-            t = t2[(b, n)]
-            s = work.tile([P, 1], F32, name="ss%d_%d" % (b, n), tag="ss", bufs=8)
-            nc.scalar.activation(out=t[:], in_=t[:], func=ACT.Exp, bias=mn[(b, n)][:, 0:1], scale=-1.0,
-                                 accum_out=s[:])
-            ssum[(b, n)] = s
+            nc.scalar.activation(out=sl(t2[b], n), in_=sl(t2[b], n), func=ACT.Exp, bias=mn[b][:, n : n + 1], scale=-1.0,
+                                 accum_out=ssum[b][:, n : n + 1])
 
-        def R(b, n):
-            r = work.tile([P, 1], F32, name="rs%d_%d" % (b, n), tag="rs", bufs=8)
-            nc.vector.reciprocal(out=r[:], in_=ssum[(b, n)][:])
-            rs[(b, n)] = r
+        def R(b, n0, c):
+            nc.vector.reciprocal(out=rs[b][:, n0 : n0 + c], in_=ssum[b][:, n0 : n0 + c])
 
         def I(b, n, eng):
-            t = t2[(b, n)]
-            r = rs[(b, n)]
+            t = sl(t2[b], n)
+            r = rs[b][:, n : n + 1]
             if eng == "s":
-                nc.scalar.activation(out=t[:], in_=t[:], func=ACT.Copy, scale=r[:, 0:1])
+                nc.scalar.activation(out=t, in_=t, func=ACT.Copy, scale=r)
             elif eng == "g":
-                nc.gpsimd.tensor_scalar(out=t[:], in0=t[:], scalar1=r[:, 0:1], scalar2=0.0, op0=ALU.mult, op1=ALU.add)
+                nc.gpsimd.tensor_scalar(out=t, in0=t, scalar1=r, scalar2=0.0, op0=ALU.mult, op1=ALU.add)
             else:
-                nc.vector.tensor_scalar(out=t[:], in0=t[:], scalar1=r[:, 0:1], scalar2=None, op0=ALU.mult)
+                nc.vector.tensor_scalar(out=t, in0=t, scalar1=r, scalar2=None, op0=ALU.mult)
 
-        def ST(b, n):
-            nc.sync.dma_start(out=out[b].rearrange("(r n) j -> r n j", n=4)[:, n, :], in_=t2[(b, n)][:])
+        def ST(b, n0, c):
+            nc.sync.dma_start(out=out[b].rearrange("(r n) j -> r n j", n=4)[:, n0 : n0 + c, :],
+                              in_=sl(t2[b], n0, c).rearrange("p (n j) -> p n j", n=c))
 
         T(0); T(2); EV(0, "s"); T(3); EV(2, "s"); T(1)
-        EV(3, "s"); QZ(2); T(4); EXPW(); EV(1, "s"); QZ(3)
-        T(6); EV(4, "s"); QZ(1); T(7); QZ(0); EV(6, "s")
-        QZ(4); T(5); WC(); EV(7, "s"); QZ(6); PJ(0, 3)
-        EV(5, "s"); QZ(7); PJ(0, 1); PJ(0, 2); TH(0, 3); QZ(5)
-        PJ(0, 0); T(9); TH(0, 2); T(8); TH(0, 1); EV(9, "v")
-        PJ(1, 2); TH(0, 0); PJ(1, 0); QZ(9); PJ(1, 3); TH(1, 2)
-        EV(8, "v"); PJ(1, 1); T(11); TH(1, 0); QZ(8); TH(1, 3)
-        T(10); EV(11, "v"); TH(1, 1); PJ(2, 2); EV(10, "v"); PJ(2, 0)
-        TH(2, 2); PJ(2, 1); PJ(2, 3); QZ(10); TH(2, 1); TQ(0, 0)
-        RG(1); TH(2, 0); TQ(0, 3); SQ(0, 0); TQ(0, 2); QZ(11)
-        RG(0); SQ(0, 3); TQ(0, 1); SQ(0, 2); PJ(3, 3); PJ(3, 2)
-        QG(1); TH(2, 3); PJ(3, 0); QG(0); SQ(0, 1); PJ(3, 1)
-        TQ(1, 3); RG(2); TH(3, 2); TQ(1, 2); TH(3, 0); TQ(1, 0)
-        NC(0); TH(3, 3); QG(2); PW(0); TQ(1, 1); TH(3, 1)
-        BK(0); SQ(1, 3); RG(3); TQ(2, 2); SQ(1, 2); D(0, 3)
-        SQ(1, 0); QG(3); D(0, 0); BR(0); SQ(1, 1); D(0, 1)
-        CK(0, "s"); NC(1); D(0, 2); TQ(2, 0); PW(1); SQ(2, 2)
-        A(0, 3); TQ(3, 1); CR(0, "s"); A(0, 0); TQ(2, 3); B(0, 3)
-        DG(0, 3, "v"); B(0, 0); C(0, 3); A(0, 1); A(0, 2); DG(0, 0, "v")
-        B(0, 1); E(0, 3); DG(0, 1, "v"); E(0, 0); TQ(2, 1); C(0, 0)
-        DG(0, 2, "v"); F(0, 3, "v"); TQ(3, 0); SQ(2, 0); E(0, 1); D(1, 1)
-        SQ(2, 1); B(0, 2); TQ(3, 2); SQ(2, 3); E(0, 2); C(0, 2)
-        F(0, 0, "v"); TQ(3, 3); SQ(3, 1); NC(2); F(0, 2, "v"); PW(2)
-        BK(1); SQ(3, 0); M(0, 0); D(1, 2); SQ(3, 2); D(1, 3)
-        M(0, 2); D(1, 0); CK(1, "s"); BR(1); M(0, 3); SQ(3, 3)
-        A(1, 2); C(0, 1); NC(3); A(1, 3); CR(1, "s"); PW(3)
-        A(1, 1); B(1, 2); F(0, 1, "v"); DG(1, 2, "v"); B(1, 1); A(1, 0)
-        C(1, 1); DG(1, 0, "v"); B(1, 3); C(1, 2); E(1, 2); C(1, 3)
-        DG(1, 1, "v"); B(1, 0); M(0, 1); C(1, 0); DG(1, 3, "v"); F(1, 2, "v")
-        H(0, 0); E(1, 0); E(1, 3); E(1, 1); M(1, 2); H(0, 1)
-        F(1, 0, "v"); H(0, 3); F(1, 1, "v"); H(1, 2); M(1, 0); H(0, 2)
-        R(0, 3); R(0, 1); R(0, 0); F(1, 3, "v"); H(1, 0); R(1, 2)
-        I(0, 0, "v"); I(0, 1, "v"); ST(0, 0); I(1, 2, "v"); R(1, 0); M(1, 1)
-        ST(1, 2); ST(0, 1); I(1, 0, "v"); H(1, 1); M(1, 3); ST(1, 0)
-        I(0, 3, "v"); H(1, 3); R(0, 2); R(1, 1); ST(0, 3); I(0, 2, "v")
-        I(1, 1, "v"); ST(0, 2); R(1, 3); ST(1, 1); I(1, 3, "v"); ST(1, 3)
+        EV(3, "s"); QH(2); QH(0); T(4); EV(1, "s"); QH(3)
+        T(6); EV(4, "s"); QH(1); T(7); EV(6, "s"); T(5)
+        EV(7, "s"); QH(6); QH(4); PJ(0, 1); EV(5, "s"); PJ(0, 3)
+        QH(7); PJ(0, 2); EXPW(); TH(0, 1); QH(5); PJ(0, 0)
+        PJ(1, 0); WC(); TH(0, 3); PJ(1, 1); PJ(1, 3); TH(0, 2)
+        PJ(1, 2); T(8); TH(0, 0); T(9); TH(1, 1); EV(8, "v")
+        TQ(0, 0); TH(1, 2); RG(0); TH(1, 0); TQ(0, 3); TH(1, 3)
+        TQ(0, 1); QG(0); SQ(0, 0); TQ(1, 3); QH(8); EV(9, "v")
+        SQ(0, 3); TQ(0, 2); SQ(0, 1); QH(9); TQ(1, 0); SQ(0, 2)
+        TQ(1, 1); SQ(1, 3); NC(0, "v"); TQ(1, 2); RG(1); PW(0)
+        SQ(1, 0); T(10); SQ(1, 1); PJ(2, 0); EV(10, "v"); T(11)
+        SQ(1, 2); QH(10); PJ(2, 3); TH(2, 0); NC(1, "v"); PJ(2, 2)
+        EV(11, "v"); PW(1); PJ(2, 1); TH(2, 3); BK(0); QH(11)
+        TH(2, 1); QG(1); BR(0); TH(2, 2); PJ(3, 0); CK(0, "s")
+        PJ(3, 3); RG(2); D(0, 3); CR(0, "s"); PJ(3, 1); PJ(3, 2)
+        TH(3, 1); D(0, 0); A(0, 3); DG(0, 3, "g"); TQ(2, 3); TH(3, 3)
+        A(0, 0); TQ(2, 0); TH(3, 0); DG(0, 0, "g"); QG(2); TH(3, 2)
+        TQ(2, 2); E(0, 3); DG(0, 2, "g"); SQ(2, 0); TQ(2, 1); B(0, 0)
+        RG(3); SQ(2, 3); TQ(3, 1); DG(0, 1, "g"); SQ(2, 1); TQ(3, 3)
+        E(0, 0); SQ(2, 2); D(0, 2); QG(3); D(0, 1); SQ(3, 1)
+        TQ(3, 2); NC(2, "v"); SQ(3, 3); A(0, 2); PW(2); TQ(3, 0)
+        SQ(3, 2); A(0, 1); BK(1); SQ(3, 0); E(0, 2); D(1, 1)
+        D(1, 0); E(0, 1); CK(1, "s"); D(1, 2); D(1, 3); C(0, 0, 1)
+        B(0, 3); BR(1); B(0, 2); B(0, 1); NC(3, "v"); A(1, 2)
+        PW(3); A(1, 3); A(1, 1); CR(1, "s"); A(1, 0); C(0, 3, 1)
+        DG(1, 1, "g"); B(1, 3); C(0, 1, 1); F(0, 0, 1, "v"); C(0, 2, 1); B(1, 1)
+        DG(1, 3, "g"); F(0, 3, 1, "v"); C(1, 1, 1); B(1, 0); DG(1, 2, "g"); C(1, 3, 1)
+        M(0, 0, 1); C(1, 0, 1); F(0, 2, 1, "v"); DG(1, 0, "g"); E(1, 1); B(1, 2)
+        E(1, 3); C(1, 2, 1); F(0, 1, 1, "v"); H(0, 0); E(1, 2); M(0, 3, 1)
+        M(0, 1, 1); M(0, 2, 1); H(0, 3); F(1, 2, 1, "v"); H(0, 1); F(1, 1, 1, "v")
+        H(0, 2); M(1, 2, 1); R(0, 1, 1); E(1, 0); R(0, 0, 1); R(0, 3, 1)
+        M(1, 1, 1); I(0, 0, "v"); H(1, 1); F(1, 3, 1, "v"); H(1, 2); R(0, 2, 1)
+        I(0, 3, "v"); M(1, 3, 1); ST(0, 3, 1); ST(0, 0, 1); R(1, 1, 1); I(0, 1, "v")
+        H(1, 3); R(1, 2, 1); I(1, 1, "v"); ST(0, 1, 1); F(1, 0, 1, "v"); ST(1, 1, 1)
+        I(0, 2, "v"); M(1, 0, 1); ST(0, 2, 1); I(1, 2, "v"); H(1, 0); R(1, 3, 1)
+        ST(1, 2, 1); I(1, 3, "v"); R(1, 0, 1); ST(1, 3, 1); I(1, 0, "v"); ST(1, 0, 1)

@@ -63,7 +63,11 @@ def tile_adaptiveattention_pa_kernel(tc, query, key, Wq, bq, Wk, bk, scoring_wei
         ident = keep.tile([P, P], F32, name="ident")
         make_identity(nc, ident[:])
         mhalf = keep.tile([P, 4], F32, name="mhalf")
-        nc.vector.memset(mhalf[:], -0.5)
+        nc.gpsimd.memset(mhalf[:], -0.5)
+        mone = keep.tile([P, 1], F32, name="mone")
+        nc.gpsimd.memset(mone[:], -1.0)
+        tiny = keep.tile([P, 1], F32, name="tiny")
+        nc.gpsimd.memset(tiny[:], 1e-15)
 
         bias_f = [keep.tile([P, 4], F32, name="bias_f%d" % s) for s in range(2)]
         wf = keep.tile([P, 3], F32, name="wf")
@@ -81,7 +85,7 @@ def tile_adaptiveattention_pa_kernel(tc, query, key, Wq, bq, Wk, bk, scoring_wei
         wsum = keep.tile([P, 1], F32, name="wsum")
         rws = keep.tile([P, 1], F32, name="rws")
         cst = keep.tile([P, 8], F32, name="cst")
-        W0, W1, W2, W2SQ, M2W2, CC = 0, 1, 2, 3, 4, 5
+        W0, W1, W2, W2SQ, CC = 0, 1, 2, 3, 4
 
         def col(c):
             return cst[:, c : c + 1]
@@ -90,12 +94,11 @@ def tile_adaptiveattention_pa_kernel(tc, query, key, Wq, bq, Wk, bk, scoring_wei
             nc.scalar.activation(out=we[:], in_=wd[:], func=ACT.Exp, accum_out=wsum[:])
 
         def WC():
-            nc.vector.reciprocal(out=rws[:], in_=wsum[:])
-            nc.vector.tensor_scalar(out=cst[:, 0:3], in0=we[:], scalar1=rws[:, 0:1], scalar2=None, op0=ALU.mult)
-            nc.vector.tensor_tensor(out=col(W2SQ), in0=col(W2), in1=col(W2), op=ALU.mult)
-            nc.vector.tensor_scalar(out=col(M2W2), in0=col(W2SQ), scalar1=-2.0, scalar2=None, op0=ALU.mult)
-            nc.vector.tensor_scalar(out=col(CC), in0=col(W1), scalar1=1e8, scalar2=col(W0),
-                                    op0=ALU.mult, op1=ALU.add)
+            g = nc.gpsimd
+            g.tensor_tensor(out=rws[:], in0=wsum[:], in1=mone[:], op=ALU.pow)
+            g.tensor_scalar(out=cst[:, 0:3], in0=we[:], scalar1=rws[:, 0:1], scalar2=0.0, op0=ALU.mult, op1=ALU.add)
+            g.tensor_tensor(out=col(W2SQ), in0=col(W2), in1=col(W2), op=ALU.mult)
+            g.tensor_scalar(out=col(CC), in0=col(W1), scalar1=1e8, scalar2=col(W0), op0=ALU.mult, op1=ALU.add)
 
         in_c = [keep.tile([P, 512], U32, name="in_c%d" % o, align_bytes=64) for o in range(6)]
         in_s = [keep.tile([P, 512], U8, name="in_s%d" % o, align_bytes=64) for o in range(6)]
@@ -161,10 +164,7 @@ def tile_adaptiveattention_pa_kernel(tc, query, key, Wq, bq, Wk, bk, scoring_wei
 
         tq = {}
         n2 = [keep.tile([P, 4], F32, name="n2_%d" % g) for g in range(4)]
-        n2c = [keep.tile([P, 4], F32, name="n2c%d" % g) for g in range(4)]
-        n2w = [keep.tile([P, 4], F32, name="n2w%d" % g) for g in range(4)]
         rn = [keep.tile([P, 4], F32, name="rn%d" % g) for g in range(4)]
-        w1rq = [keep.tile([P, 4], F32, name="w1rq%d" % b) for b in range(2)]
 
         def TQ(g, n):
             a = bank("tq%d_%d" % (g, n), "tq")
@@ -175,20 +175,13 @@ def tile_adaptiveattention_pa_kernel(tc, query, key, Wq, bq, Wk, bk, scoring_wei
 
         def SQ(g, n):
             j = work.tile([P, 512], BF16, name="jk%d_%d" % (g, n), tag="junk", bufs=BUFS["junk"])
-            nc.scalar.activation(out=j[:], in_=tq[(g, n)][:], func=ACT.Square, accum_out=n2[g][:, n : n + 1])
-
-        def NC(g, eng):
-            e = nc.gpsimd if eng == "g" else nc.vector
-            e.tensor_scalar(out=n2c[g][:], in0=n2[g][:], scalar1=TINY, scalar2=1.0, op0=ALU.max, op1=ALU.mult)
-            e.tensor_scalar(out=n2w[g][:], in0=n2[g][:], scalar1=TINY, scalar2=col(W2SQ), op0=ALU.max, op1=ALU.mult)
+            nc.scalar.activation(out=j[:], in_=tq[(g, n)][:], func=ACT.Square, bias=tiny[:, 0:1],
+                                 accum_out=n2[g][:, n : n + 1])
 
         def PW(g):
-            nc.gpsimd.tensor_tensor(out=rn[g][:], in0=n2c[g][:], in1=mhalf[:], op=ALU.pow)
-            if g % 2 == 1:
-                nc.gpsimd.tensor_scalar(out=w1rq[g // 2][:], in0=rn[g][:], scalar1=col(W1), scalar2=0.0,
-                                        op0=ALU.mult, op1=ALU.add)
+            nc.gpsimd.tensor_tensor(out=rn[g][:], in0=n2[g][:], in1=mhalf[:], op=ALU.pow)
 
-        kn2w_sb = [keep.tile([P, 512], F32, name="kn2w_sb%d" % b) for b in range(2)]
+        kn2_sb = [keep.tile([P, 512], F32, name="kn2_sb%d" % b) for b in range(2)]
         rkb_sb = [keep.tile([P, 512], F32, name="rkb_sb%d" % b) for b in range(2)]
         bc = {}
 
@@ -199,16 +192,16 @@ def tile_adaptiveattention_pa_kernel(tc, query, key, Wq, bq, Wk, bk, scoring_wei
             return a
 
         def BK(b):
-            bc[("k", b)] = spread("bck%d" % b, n2w[2 * b])
+            bc[("k", b)] = spread("bck%d" % b, n2[2 * b])
 
         def BR(b):
             bc[("r", b)] = spread("bcr%d" % b, rn[2 * b])
 
         def CK(b, eng):
-            ew_copy(eng, kn2w_sb[b][:], bc[("k", b)][:])
+            ew_copy(eng, kn2_sb[b][:], bc[("k", b)][:])
 
         def CR(b, eng):
-            ew_copy(eng, rkb_sb[b][:], bc[("r", b)][:])
+            nc.scalar.activation(out=rkb_sb[b][:], in_=bc[("r", b)][:], func=ACT.Copy, scale=col(W1))
 
         dot = {}
         gp = {}
@@ -231,27 +224,27 @@ def tile_adaptiveattention_pa_kernel(tc, query, key, Wq, bq, Wk, bk, scoring_wei
             dot[(b, n)] = a
 
         def A(b, n):
-            nc.vector.scalar_tensor_tensor(out=sl(zt[b], n), in0=dot[(b, n)][:], scalar=col(M2W2), in1=kn2w_sb[b][:],
+            nc.vector.scalar_tensor_tensor(out=sl(zt[b], n), in0=dot[(b, n)][:], scalar=-2.0, in1=kn2_sb[b][:],
                                            op0=ALU.mult, op1=ALU.add)
 
         def B(b, n):
-            nc.vector.tensor_scalar(out=sl(zt[b], n), in0=sl(zt[b], n), scalar1=n2w[2 * b + 1][:, n : n + 1],
-                                    scalar2=TINY, op0=ALU.add, op1=ALU.max)
+            nc.vector.tensor_scalar(out=sl(zt[b], n), in0=sl(zt[b], n), scalar1=n2[2 * b + 1][:, n : n + 1],
+                                    scalar2=0.0, op0=ALU.add, op1=ALU.max)
 
         def C(b, n0, c):
-            nc.scalar.activation(out=sl(zt[b], n0, c), in_=sl(zt[b], n0, c), func=ACT.Sqrt)
+            nc.scalar.activation(out=sl(zt[b], n0, c), in_=sl(zt[b], n0, c), func=ACT.Sqrt, scale=col(W2SQ))
 
         def DG(b, n, eng="g"):
             g = work.tile([P, 512], F32, name="gp%d_%d" % (b, n), tag="gp", bufs=BUFS["gp"])
             if eng == "g":
-                nc.gpsimd.tensor_scalar(out=g[:], in0=rkb_sb[b][:], scalar1=w1rq[b][:, n : n + 1], scalar2=col(W0),
+                nc.gpsimd.tensor_scalar(out=g[:], in0=rkb_sb[b][:], scalar1=rn[2 * b + 1][:, n : n + 1], scalar2=col(W0),
                                         op0=ALU.mult, op1=ALU.add)
             elif eng == "v":
-                nc.vector.tensor_scalar(out=g[:], in0=rkb_sb[b][:], scalar1=w1rq[b][:, n : n + 1], scalar2=col(W0),
+                nc.vector.tensor_scalar(out=g[:], in0=rkb_sb[b][:], scalar1=rn[2 * b + 1][:, n : n + 1], scalar2=col(W0),
                                         op0=ALU.mult, op1=ALU.add)
             else:
                 nc.scalar.activation(out=g[:], in_=rkb_sb[b][:], func=ACT.Identity, bias=col(W0),
-                                     scale=w1rq[b][:, n : n + 1])
+                                     scale=rn[2 * b + 1][:, n : n + 1])
             gp[(b, n)] = g
 
         def E(b, n):
@@ -297,9 +290,9 @@ def tile_adaptiveattention_pa_kernel(tc, query, key, Wq, bq, Wk, bk, scoring_wei
         TQ(0, 0); TH(1, 2); RG(0); TH(1, 0); TQ(0, 3); TH(1, 3)
         TQ(0, 1); QG(0); SQ(0, 0); TQ(1, 3); QH(8); EV(9, "v")
         SQ(0, 3); TQ(0, 2); SQ(0, 1); QH(9); TQ(1, 0); SQ(0, 2)
-        TQ(1, 1); SQ(1, 3); NC(0, "v"); TQ(1, 2); RG(1); PW(0)
+        TQ(1, 1); SQ(1, 3); TQ(1, 2); RG(1); PW(0)
         SQ(1, 0); T(10); SQ(1, 1); PJ(2, 0); EV(10, "v"); T(11)
-        SQ(1, 2); QH(10); PJ(2, 3); TH(2, 0); NC(1, "v"); PJ(2, 2)
+        SQ(1, 2); QH(10); PJ(2, 3); TH(2, 0); PJ(2, 2)
         EV(11, "v"); PW(1); PJ(2, 1); TH(2, 3); BK(0); QH(11)
         TH(2, 1); QG(1); BR(0); TH(2, 2); PJ(3, 0); CK(0, "s")
         PJ(3, 3); RG(2); D(0, 3); CR(0, "s"); PJ(3, 1); PJ(3, 2)
@@ -308,10 +301,10 @@ def tile_adaptiveattention_pa_kernel(tc, query, key, Wq, bq, Wk, bk, scoring_wei
         TQ(2, 2); E(0, 3); DG(0, 2, "g"); SQ(2, 0); TQ(2, 1); B(0, 0)
         RG(3); SQ(2, 3); TQ(3, 1); DG(0, 1, "g"); SQ(2, 1); TQ(3, 3)
         E(0, 0); SQ(2, 2); D(0, 2); QG(3); D(0, 1); SQ(3, 1)
-        TQ(3, 2); NC(2, "v"); SQ(3, 3); A(0, 2); PW(2); TQ(3, 0)
+        TQ(3, 2); SQ(3, 3); A(0, 2); PW(2); TQ(3, 0)
         SQ(3, 2); A(0, 1); BK(1); SQ(3, 0); E(0, 2); D(1, 1)
         D(1, 0); E(0, 1); CK(1, "s"); D(1, 2); D(1, 3); C(0, 0, 1)
-        B(0, 3); BR(1); B(0, 2); B(0, 1); NC(3, "v"); A(1, 2)
+        B(0, 3); BR(1); B(0, 2); B(0, 1); A(1, 2)
         PW(3); A(1, 3); A(1, 1); CR(1, "s"); A(1, 0); C(0, 3, 1)
         DG(1, 1, "g"); B(1, 3); C(0, 1, 1); F(0, 0, 1, "v"); C(0, 2, 1); B(1, 1)
         DG(1, 3, "g"); F(0, 3, 1, "v"); C(1, 1, 1); B(1, 0); DG(1, 2, "g"); C(1, 3, 1)

@@ -16,7 +16,7 @@ AX = mybir.AxisListType
 
 P = 128
 TINY = 1e-30
-BUFS = {"f":3,"gq":2,"gp":8,"junk":2}
+BUFS = {"f":4,"gq":2,"gp":8,"junk":2}
 
 
 def tile_adaptiveattention_pa_kernel(tc, query, key, Wq, bq, Wk, bk, scoring_weights, out):
@@ -178,8 +178,21 @@ def tile_adaptiveattention_pa_kernel(tc, query, key, Wq, bq, Wk, bk, scoring_wei
             nc.scalar.activation(out=j[:], in_=tq[(g, n)][:], func=ACT.Square, bias=tiny[:, 0:1],
                                  accum_out=n2[g][:, n : n + 1])
 
-        def PW(g):
-            nc.gpsimd.tensor_tensor(out=rn[g][:], in0=n2[g][:], in1=mhalf[:], op=ALU.pow)
+        def KD(g, n):
+            a = bank("kd%d_%d" % (g, n), "tq")
+            for t in range(4):
+                x = ft[g][:, t * 512 + n * 128 : t * 512 + n * 128 + 128]
+                nc.tensor.matmul(a[:, 0:128], lhsT=x, rhs=x, start=(t == 0), stop=(t == 3))
+            tq[(g, n)] = a
+
+        def KE(g, n):
+            j = work.tile([P, P], F32, name="kj%d_%d" % (g, n), tag="kj", bufs=2)
+            nc.vector.scalar_tensor_tensor(out=j[:], in0=tq[(g, n)][:, 0:128], scalar=TINY, in1=ident[:],
+                                           op0=ALU.max, op1=ALU.mult, accum_out=n2[g][:, n : n + 1])
+
+        def PW(g, n0=0, c=4):
+            nc.gpsimd.tensor_tensor(out=rn[g][:, n0 : n0 + c], in0=n2[g][:, n0 : n0 + c], in1=mhalf[:, 0:c],
+                                    op=ALU.pow)
 
         kn2_sb = [keep.tile([P, 512], F32, name="kn2_sb%d" % b) for b in range(2)]
         rkb_sb = [keep.tile([P, 512], F32, name="rkb_sb%d" % b) for b in range(2)]
@@ -280,40 +293,99 @@ def tile_adaptiveattention_pa_kernel(tc, query, key, Wq, bq, Wk, bk, scoring_wei
             nc.sync.dma_start(out=out[b].rearrange("(r n) j -> r n j", n=4)[:, n0 : n0 + c, :],
                               in_=sl(t2[b], n0, c).rearrange("p (n j) -> p n j", n=c))
 
-        T(0); T(2); EV(0, "s"); T(3); EV(2, "s"); T(1)
-        EV(3, "s"); QH(2); QH(0); T(4); EV(1, "s"); QH(3)
-        T(6); EV(4, "s"); QH(1); T(7); EV(6, "s"); T(5)
-        EV(7, "s"); QH(6); QH(4); PJ(0, 1); EV(5, "s"); PJ(0, 3)
-        QH(7); PJ(0, 2); EXPW(); TH(0, 1); QH(5); PJ(0, 0)
-        PJ(1, 0); WC(); TH(0, 3); PJ(1, 1); PJ(1, 3); TH(0, 2)
-        PJ(1, 2); T(8); TH(0, 0); T(9); TH(1, 1); EV(8, "v")
-        TQ(0, 0); TH(1, 2); RG(0); TH(1, 0); TQ(0, 3); TH(1, 3)
-        TQ(0, 1); QG(0); SQ(0, 0); TQ(1, 3); QH(8); EV(9, "v")
-        SQ(0, 3); TQ(0, 2); SQ(0, 1); QH(9); TQ(1, 0); SQ(0, 2)
-        TQ(1, 1); SQ(1, 3); TQ(1, 2); RG(1); PW(0)
-        SQ(1, 0); T(10); SQ(1, 1); PJ(2, 0); EV(10, "v"); T(11)
-        SQ(1, 2); QH(10); PJ(2, 3); TH(2, 0); PJ(2, 2)
-        EV(11, "v"); PW(1); PJ(2, 1); TH(2, 3); BK(0); QH(11)
-        TH(2, 1); QG(1); BR(0); TH(2, 2); PJ(3, 0); CK(0, "s")
-        PJ(3, 3); RG(2); D(0, 3); CR(0, "s"); PJ(3, 1); PJ(3, 2)
-        TH(3, 1); D(0, 0); A(0, 3); DG(0, 3, "g"); TQ(2, 3); TH(3, 3)
-        A(0, 0); TQ(2, 0); TH(3, 0); DG(0, 0, "g"); QG(2); TH(3, 2)
-        TQ(2, 2); E(0, 3); DG(0, 2, "g"); SQ(2, 0); TQ(2, 1); B(0, 0)
-        RG(3); SQ(2, 3); TQ(3, 1); DG(0, 1, "g"); SQ(2, 1); TQ(3, 3)
-        E(0, 0); SQ(2, 2); D(0, 2); QG(3); D(0, 1); SQ(3, 1)
-        TQ(3, 2); SQ(3, 3); A(0, 2); PW(2); TQ(3, 0)
-        SQ(3, 2); A(0, 1); BK(1); SQ(3, 0); E(0, 2); D(1, 1)
-        D(1, 0); E(0, 1); CK(1, "s"); D(1, 2); D(1, 3); C(0, 0, 1)
-        B(0, 3); BR(1); B(0, 2); B(0, 1); A(1, 2)
-        PW(3); A(1, 3); A(1, 1); CR(1, "s"); A(1, 0); C(0, 3, 1)
-        DG(1, 1, "g"); B(1, 3); C(0, 1, 1); F(0, 0, 1, "v"); C(0, 2, 1); B(1, 1)
-        DG(1, 3, "g"); F(0, 3, 1, "v"); C(1, 1, 1); B(1, 0); DG(1, 2, "g"); C(1, 3, 1)
-        M(0, 0, 1); C(1, 0, 1); F(0, 2, 1, "v"); DG(1, 0, "g"); E(1, 1); B(1, 2)
-        E(1, 3); C(1, 2, 1); F(0, 1, 1, "v"); H(0, 0); E(1, 2); M(0, 3, 1)
-        M(0, 1, 1); M(0, 2, 1); H(0, 3); F(1, 2, 1, "v"); H(0, 1); F(1, 1, 1, "v")
-        H(0, 2); M(1, 2, 1); R(0, 1, 1); E(1, 0); R(0, 0, 1); R(0, 3, 1)
-        M(1, 1, 1); I(0, 0, "v"); H(1, 1); F(1, 3, 1, "v"); H(1, 2); R(0, 2, 1)
-        I(0, 3, "v"); M(1, 3, 1); ST(0, 3, 1); ST(0, 0, 1); R(1, 1, 1); I(0, 1, "v")
-        H(1, 3); R(1, 2, 1); I(1, 1, "v"); ST(0, 1, 1); F(1, 0, 1, "v"); ST(1, 1, 1)
-        I(0, 2, "v"); M(1, 0, 1); ST(0, 2, 1); I(1, 2, "v"); H(1, 0); R(1, 3, 1)
-        ST(1, 2, 1); I(1, 3, "v"); R(1, 0, 1); ST(1, 3, 1); I(1, 0, "v"); ST(1, 0, 1)
+
+        IN0 = (0, 2, 3, 1, 4, 6, 7, 5)
+        for k, i in enumerate(IN0):
+            T(i)
+            EV(i, "v" if k in (1, 5) else "s")
+            if k:
+                QH(IN0[k - 1])
+        EXPW(); WC()
+        for t in range(2):
+            PJ(0, t)
+        QH(5)
+        for t in range(2, 4):
+            PJ(0, t)
+        T(8); T(9); T(10); T(11)
+        EV(8, "v"); EV(9, "v"); QH(8); QH(9)
+        for t in range(4):
+            TH(0, t)
+        for t in range(4):
+            PJ(1, t)
+        EV(11, "s")
+        RG(0)
+        EV(10, "v"); QG(0)
+        QH(10); QH(11)
+        KD(0, 0)
+        for t in range(4):
+            TH(1, t)
+        for t in range(4):
+            PJ(2, t)
+        KD(0, 1)
+        KE(0, 0)
+        for t in range(4):
+            TH(2, t)
+        for t in range(4):
+            PJ(3, t)
+        KD(0, 2)
+        RG(1); KE(0, 1); QG(1)
+        TQ(0, 3)
+        for t in range(4):
+            TH(3, t)
+        SQ(0, 3)
+        for n in range(4):
+            TQ(1, n)
+        RG(2); KE(0, 2)
+        PW(0); BK(0)
+        for n in range(4):
+            D(0, n)
+        SQ(1, 0); CK(0, "s"); SQ(1, 1)
+        BR(0)
+        SQ(1, 2); SQ(1, 3); CR(0, "s")
+        QG(2)
+        RG(3)
+        QG(3)
+        for n in range(4):
+            A(0, n)
+        PW(1)
+        DG(0, 0, "g"); DG(0, 1, "g")
+        for n in range(4):
+            TQ(2, n); SQ(2, n)
+        for n in range(4):
+            B(0, n)
+            C(0, n, 1)
+        PW(2); BK(1)
+        DG(0, 2, "v"); DG(0, 3, "v")
+        for n in (2, 3, 0, 1):
+            E(0, n); D(1, n)
+        CK(1, "s")
+        for n in range(4):
+            TQ(3, n); SQ(3, n)
+        PW(3); BR(1); CR(1, "s")
+        for n in range(4):
+            F(0, n, 1)
+        M(0, 0, 1)
+        for n in range(4):
+            A(1, n); DG(1, n, "g")
+        for n in range(4):
+            B(1, n); C(1, n, 1)
+        M(0, 1, 1); M(0, 2, 1); M(0, 3, 1)
+        for n in range(4):
+            H(0, n)
+        E(1, 0); E(1, 1); F(1, 0, 1); F(1, 1, 1); M(1, 0, 1); M(1, 1, 1)
+        R(0, 0, 2)
+        I(0, 0, "s"); ST(0, 0, 1); I(0, 1, "s"); ST(0, 1, 1)
+        H(1, 0); H(1, 1)
+        E(1, 2); E(1, 3); F(1, 2, 1); F(1, 3, 1)
+        R(0, 2, 2)
+        M(1, 2, 1)
+        I(0, 2, "v"); ST(0, 2, 1)
+        M(1, 3, 1)
+        H(1, 2); H(1, 3)
+        I(0, 3, "v"); ST(0, 3, 1)
+        R(1, 0, 2)
+        I(1, 0, "v"); ST(1, 0, 1)
+        I(1, 1, "v"); ST(1, 1, 1)
+        for n in (2, 3):
+            R(1, n, 1)
+            I(1, n, "v"); ST(1, n, 1)

@@ -155,8 +155,8 @@ def tile_adaptiveattention_pa_kernel(tc, query, key, Wq, bq, Wk, bk, scoring_wei
 
         def RG(g):
             r = work.tile([P, 2048], BF16, name="gq%d" % g, tag="gq", bufs=BUFS["gq"], align_bytes=64)
-            nc.vector.tensor_copy(out=r[:].rearrange("p (w t) -> p w t", t=4),
-                                  in_=ft[g][:].rearrange("p (t w) -> p w t", t=4))
+            nc.vector.tensor_copy(out=r[:].rearrange("p (c i t) -> p c t i", i=4, t=4),
+                                  in_=ft[g][:].rearrange("p (t c i) -> p c t i", i=4, t=4))
             gq[g] = r
 
         def QG(g):

@@ -46,7 +46,7 @@ def tile_adaptiveattention_pa_kernel(tc, query, key, Wq, bq, Wk, bk, scoring_wei
             return w.rearrange("(p t) i -> p t i", t=4)[:, 2 * h : 2 * h + 2, :]
 
         def k_src(b, h):
-            return key[b, 256 * h : 256 * h + 256, :].rearrange("(n p) i -> p n i", p=P)
+            return key[b, 256 * h : 256 * h + 256, :].rearrange("(p n) i -> p n i", n=2)
 
         def q_src(b, h):
             return query[b].rearrange("(p n) i -> p n i", n=4)[:, 2 * h : 2 * h + 2, :]
@@ -118,8 +118,12 @@ def tile_adaptiveattention_pa_kernel(tc, query, key, Wq, bq, Wk, bk, scoring_wei
             o, h = i // 2, i % 2
             if o not in grp:
                 grp[o] = keep.tile([P, 2048], BF16, name="grp%d" % o, align_bytes=64)
-            ew_copy(eng, grp[o][:, 1024 * h : 1024 * h + 1024].bitcast(F32).rearrange("p (r u) -> p r u", u=2),
-                    xt[i][:].rearrange("p (u r) -> p r u", u=2))
+            words = grp[o][:, 1024 * h : 1024 * h + 1024].bitcast(F32)
+            if o in (1, 4):
+                ew_copy(eng, words.rearrange("p (r n u) -> p r n u", n=2, u=2),
+                        xt[i][:].rearrange("p (u n r) -> p r n u", n=2, u=2))
+            else:
+                ew_copy(eng, words.rearrange("p (r u) -> p r u", u=2), xt[i][:].rearrange("p (u r) -> p r u", u=2))
 
         def QH(i):
             o, h = i // 2, i % 2

@@ -64,8 +64,6 @@ def tile_adaptiveattention_pa_kernel(tc, query, key, Wq, bq, Wk, bk, scoring_wei
         make_identity(nc, ident[:])
         mhalf = keep.tile([P, 4], F32, name="mhalf")
         nc.gpsimd.memset(mhalf[:], -0.5)
-        mone = keep.tile([P, 1], F32, name="mone")
-        nc.gpsimd.memset(mone[:], -1.0)
         tiny = keep.tile([P, 1], F32, name="tiny")
         nc.gpsimd.memset(tiny[:], 1e-15)
 
@@ -93,12 +91,16 @@ def tile_adaptiveattention_pa_kernel(tc, query, key, Wq, bq, Wk, bk, scoring_wei
         def EXPW():
             nc.scalar.activation(out=we[:], in_=wd[:], func=ACT.Exp, accum_out=wsum[:])
 
-        def WC():
-            g = nc.gpsimd
-            g.tensor_tensor(out=rws[:], in0=wsum[:], in1=mone[:], op=ALU.pow)
-            g.tensor_scalar(out=cst[:, 0:3], in0=we[:], scalar1=rws[:, 0:1], scalar2=0.0, op0=ALU.mult, op1=ALU.add)
-            g.tensor_tensor(out=col(W2SQ), in0=col(W2), in1=col(W2), op=ALU.mult)
-            g.tensor_scalar(out=col(CC), in0=col(W1), scalar1=1e8, scalar2=col(W0), op0=ALU.mult, op1=ALU.add)
+        def WC(step):
+            v = nc.vector
+            if step == 0:
+                v.reciprocal(out=rws[:], in_=wsum[:])
+            elif step == 1:
+                v.tensor_scalar(out=cst[:, 0:3], in0=we[:], scalar1=rws[:, 0:1], scalar2=None, op0=ALU.mult)
+            elif step == 2:
+                v.tensor_tensor(out=col(W2SQ), in0=col(W2), in1=col(W2), op=ALU.mult)
+            else:
+                v.tensor_scalar(out=col(CC), in0=col(W1), scalar1=1e8, scalar2=col(W0), op0=ALU.mult, op1=ALU.add)
 
         in_c = [keep.tile([P, 512], U32, name="in_c%d" % o, align_bytes=64) for o in range(6)]
         in_s = [keep.tile([P, 512], U8, name="in_s%d" % o, align_bytes=64) for o in range(6)]
@@ -197,6 +199,14 @@ def tile_adaptiveattention_pa_kernel(tc, query, key, Wq, bq, Wk, bk, scoring_wei
         def PW(g, n0=0, c=4):
             nc.gpsimd.tensor_tensor(out=rn[g][:, n0 : n0 + c], in0=n2[g][:, n0 : n0 + c], in1=mhalf[:, 0:c],
                                     op=ALU.pow)
+
+        qn = [keep.tile([P, 4], F32, name="qn%d" % g) for g in range(4)]
+
+        def SR(g):
+            nc.scalar.activation(out=qn[g][:], in_=n2[g][:], func=ACT.Sqrt)
+
+        def RV(g):
+            nc.vector.reciprocal(out=rn[g][:], in_=qn[g][:])
 
         kn2_sb = [keep.tile([P, 512], F32, name="kn2_sb%d" % b) for b in range(2)]
         rkb_sb = [keep.tile([P, 512], F32, name="rkb_sb%d" % b) for b in range(2)]
@@ -302,9 +312,12 @@ def tile_adaptiveattention_pa_kernel(tc, query, key, Wq, bq, Wk, bk, scoring_wei
         for k, i in enumerate(IN0):
             T(i)
             EV(i, "v" if k in (1, 5) else "s")
+            if k == 0:
+                EXPW()
             if k:
                 QH(IN0[k - 1])
-        EXPW(); WC()
+            if k > 3:
+                WC(k - 4)
         for t in range(2):
             PJ(0, t)
         QH(5)
@@ -316,80 +329,95 @@ def tile_adaptiveattention_pa_kernel(tc, query, key, Wq, bq, Wk, bk, scoring_wei
             TH(0, t)
         for t in range(4):
             PJ(1, t)
-        EV(11, "s")
         RG(0)
         EV(10, "v"); QG(0)
-        QH(10); QH(11)
         KD(0, 0)
         for t in range(4):
             TH(1, t)
         for t in range(4):
             PJ(2, t)
-        KD(0, 1)
+        EV(11, "s")
+        QH(10); QH(11)
+        TQ(0, 3)
+        KD(0, 1); KD(0, 2)
         KE(0, 0)
         for t in range(4):
             TH(2, t)
-        for t in range(4):
-            PJ(3, t)
-        KD(0, 2)
         RG(1); KE(0, 1); QG(1)
-        TQ(0, 3)
-        for t in range(4):
-            TH(3, t)
+        PJ(3, 0); PJ(3, 1)
         SQ(0, 3)
-        for n in range(4):
-            TQ(1, n)
-        RG(2); KE(0, 2)
+        KE(0, 2)
         PW(0); BK(0)
+        TH(3, 0); TH(3, 1)
         for n in range(4):
             D(0, n)
-        SQ(1, 0); CK(0, "s"); SQ(1, 1)
-        BR(0)
-        SQ(1, 2); SQ(1, 3); CR(0, "s")
-        QG(2)
-        RG(3)
-        QG(3)
+        CK(0, "s")
+        PJ(3, 2); PJ(3, 3)
+        TH(3, 2); TH(3, 3)
+        RG(2); QG(2)
+        for n in range(4):
+            TQ(1, n)
         for n in range(4):
             A(0, n)
-        PW(1)
-        DG(0, 0, "g"); DG(0, 1, "g")
+        SQ(1, 0); SQ(1, 1)
+        PW(1, 0, 2)
+        BR(0)
+        SQ(1, 2); SQ(1, 3)
+        PW(1, 2, 2)
+        CR(0, "s")
         for n in range(4):
-            TQ(2, n); SQ(2, n)
-        for n in range(4):
-            B(0, n)
-            C(0, n, 1)
-        PW(2); BK(1)
-        DG(0, 2, "v"); DG(0, 3, "v")
+            KD(2, n)
+        RG(3)
         for n in (2, 3, 0, 1):
-            E(0, n); D(1, n)
-        CK(1, "s")
+            B(0, n)
+        for n in (2, 3, 0, 1):
+            C(0, n, 1)
+        DG(0, 0, "g"); DG(0, 1, "g")
+        KE(2, 0); QG(3); KE(2, 1)
+        DG(0, 2, "v"); DG(0, 3, "v")
+        TQ(3, 0); TQ(3, 1)
+        E(0, 2); E(0, 3); KE(2, 2); KE(2, 3); E(0, 0); E(0, 1)
+        BK(1); CK(1, "s")
+        TQ(3, 2); TQ(3, 3)
+        for n in (2, 3, 0, 1):
+            D(1, n)
+        SR(2)
         for n in range(4):
-            TQ(3, n); SQ(3, n)
-        PW(3); BR(1); CR(1, "s")
-        for n in range(4):
-            F(0, n, 1)
-        M(0, 0, 1)
-        for n in range(4):
-            A(1, n); DG(1, n, "g")
-        for n in range(4):
+            SQ(3, n)
+        SR(3)
+        for n in (2, 3, 0, 1):
+            F(0, n, 1, "g")
+        RV(2); BR(1); CR(1, "s")
+        for n in (2, 3, 0, 1):
+            A(1, n)
+        for n in (2, 3, 0, 1):
             B(1, n); C(1, n, 1)
-        M(0, 1, 1); M(0, 2, 1); M(0, 3, 1)
-        for n in range(4):
+        RV(3)
+        for n in (0, 1, 2, 3):
+            DG(1, n, "g")
+        for n in (2, 3, 0, 1):
+            M(0, n, 1)
+        for n in (2, 3, 0, 1):
             H(0, n)
-        E(1, 0); E(1, 1); F(1, 0, 1); F(1, 1, 1); M(1, 0, 1); M(1, 1, 1)
-        R(0, 0, 2)
-        I(0, 0, "s"); ST(0, 0, 1); I(0, 1, "s"); ST(0, 1, 1)
-        H(1, 0); H(1, 1)
-        E(1, 2); E(1, 3); F(1, 2, 1); F(1, 3, 1)
+        for n in range(4):
+            E(1, n)
+        F(1, 0, 1, "g"); F(1, 1, 1, "g")
+        F(1, 2, 1)
         R(0, 2, 2)
-        M(1, 2, 1)
+        F(1, 3, 1)
         I(0, 2, "v"); ST(0, 2, 1)
-        M(1, 3, 1)
-        H(1, 2); H(1, 3)
+        M(1, 2, 1); H(1, 2)
         I(0, 3, "v"); ST(0, 3, 1)
-        R(1, 0, 2)
-        I(1, 0, "v"); ST(1, 0, 1)
-        I(1, 1, "v"); ST(1, 1, 1)
-        for n in (2, 3):
+        M(1, 3, 1); H(1, 3)
+        R(0, 0, 2)
+        M(1, 0, 1); H(1, 0)
+        I(0, 0, "v"); ST(0, 0, 1)
+        M(1, 1, 1); H(1, 1)
+        I(0, 1, "v"); ST(0, 1, 1)
+        R(1, 2, 2)
+        I(1, 2, "v"); ST(1, 2, 1)
+        I(1, 3, "v"); ST(1, 3, 1)
+        for n in (0, 1):
             R(1, n, 1)
+        for n in (0, 1):
             I(1, n, "v"); ST(1, n, 1)

@@ -329,91 +329,91 @@ def tile_adaptiveattention_pa_kernel(tc, query, key, Wq, bq, Wk, bk, scoring_wei
             TH(0, t)
         for t in range(4):
             PJ(1, t)
+        EV(11, "s")
         RG(0)
         EV(10, "v"); QG(0)
+        QH(10); QH(11)
         KD(0, 0)
         for t in range(4):
             TH(1, t)
         for t in range(4):
             PJ(2, t)
-        EV(11, "s")
-        QH(10); QH(11)
-        TQ(0, 3)
-        KD(0, 1); KD(0, 2)
+        KD(0, 1)
         KE(0, 0)
         for t in range(4):
             TH(2, t)
+        for t in range(4):
+            PJ(3, t)
+        KD(0, 2)
         RG(1); KE(0, 1); QG(1)
-        PJ(3, 0); PJ(3, 1)
+        TQ(0, 3)
+        for t in range(4):
+            TH(3, t)
         SQ(0, 3)
-        KE(0, 2)
-        PW(0); BK(0)
-        TH(3, 0); TH(3, 1)
-        for n in range(4):
-            D(0, n)
-        CK(0, "s")
-        PJ(3, 2); PJ(3, 3)
-        TH(3, 2); TH(3, 3)
-        RG(2); QG(2)
         for n in range(4):
             TQ(1, n)
+        RG(2); KE(0, 2)
+        PW(0); BK(0)
         for n in range(4):
-            A(0, n)
-        SQ(1, 0); SQ(1, 1)
+            D(0, n)
+        SQ(1, 0); CK(0, "s"); SQ(1, 1)
         PW(1, 0, 2)
         BR(0)
-        SQ(1, 2); SQ(1, 3)
+        SQ(1, 2); SQ(1, 3); CR(0, "s")
+        QG(2)
+        RG(3)
+        QG(3)
+        for n in range(4):
+            A(0, n)
         PW(1, 2, 2)
-        CR(0, "s")
         for n in range(4):
             KD(2, n)
-        RG(3)
-        for n in (2, 3, 0, 1):
+        for n in range(4):
             B(0, n)
-        for n in (2, 3, 0, 1):
+        for n in range(4):
             C(0, n, 1)
-        DG(0, 0, "g"); DG(0, 1, "g")
-        KE(2, 0); QG(3); KE(2, 1)
-        DG(0, 2, "v"); DG(0, 3, "v")
+        DG(0, 2, "g"); DG(0, 3, "g")
+        KE(2, 0); KE(2, 1)
+        DG(0, 0, "v"); DG(0, 1, "v")
         TQ(3, 0); TQ(3, 1)
-        E(0, 2); E(0, 3); KE(2, 2); KE(2, 3); E(0, 0); E(0, 1)
+        E(0, 0); KE(2, 2); E(0, 1); KE(2, 3); E(0, 2); E(0, 3)
         BK(1); CK(1, "s")
-        TQ(3, 2); TQ(3, 3)
-        for n in (2, 3, 0, 1):
+        for n in range(4):
             D(1, n)
+        TQ(3, 2); TQ(3, 3)
         SR(2)
         for n in range(4):
             SQ(3, n)
         SR(3)
-        for n in (2, 3, 0, 1):
+        for n in range(3):
             F(0, n, 1, "g")
-        RV(2); BR(1); CR(1, "s")
-        for n in (2, 3, 0, 1):
-            A(1, n)
-        for n in (2, 3, 0, 1):
+        F(0, 3, 1)
+        A(1, 0); RV(2); A(1, 1); A(1, 2); A(1, 3)
+        BR(1); CR(1, "s")
+        for n in range(4):
             B(1, n); C(1, n, 1)
         RV(3)
         for n in (0, 1, 2, 3):
             DG(1, n, "g")
-        for n in (2, 3, 0, 1):
+        for n in range(4):
             M(0, n, 1)
-        for n in (2, 3, 0, 1):
+        for n in range(4):
             H(0, n)
         for n in range(4):
             E(1, n)
         F(1, 0, 1, "g"); F(1, 1, 1, "g")
         F(1, 2, 1)
-        R(0, 2, 2)
-        F(1, 3, 1)
-        I(0, 2, "v"); ST(0, 2, 1)
-        M(1, 2, 1); H(1, 2)
-        I(0, 3, "v"); ST(0, 3, 1)
-        M(1, 3, 1); H(1, 3)
         R(0, 0, 2)
-        M(1, 0, 1); H(1, 0)
-        I(0, 0, "v"); ST(0, 0, 1)
-        M(1, 1, 1); H(1, 1)
+        F(1, 3, 1)
+        I(0, 0, "s"); ST(0, 0, 1)
+        M(1, 2, 1); H(1, 2)
         I(0, 1, "v"); ST(0, 1, 1)
+        M(1, 3, 1); H(1, 3)
+        R(0, 2, 2)
+        M(1, 0, 1); H(1, 0)
+        I(0, 2, "v"); ST(0, 2, 1)
+        M(1, 1, 1); H(1, 1)
+        I(0, 3, "v"); ST(0, 3, 1)
         R(1, 2, 2)
         I(1, 2, "v"); ST(1, 2, 1)
         I(1, 3, "v"); ST(1, 3, 1)

from contextlib import ExitStack

import concourse.mybir as mybir
from concourse.masks import make_identity

FLOPS = 2 * (2 * 1024 * 512 * 512) + 2 * 2 * 512 * 512 * 512

F32 = mybir.dt.float32
BF16 = mybir.dt.bfloat16
U32 = mybir.dt.uint32
U8 = mybir.dt.uint8
FP8X4 = mybir.dt.float8_e4m3fn_x4
ACT = mybir.ActivationFunctionType
ALU = mybir.AluOpType
AX = mybir.AxisListType

P = 128
TINY = 1e-30
BUFS = {"f":4,"gq":2,"gp":8,"junk":2}


def tile_adaptiveattention_pa_kernel(tc, query, key, Wq, bq, Wk, bk, scoring_weights, out):
    nc = tc.nc
    with ExitStack() as ctx:
        ctx.enter_context(tc.manual_schedule())
        keep = ctx.enter_context(tc.tile_pool(name="keep", bufs=1))
        work = ctx.enter_context(tc.tile_pool(name="work", bufs=2))
        psum = ctx.enter_context(tc.psum_pool(name="psum", bufs=1))

        def bank(name, tag):
            return psum.tile([P, 512], F32, name=name, tag="ps", bufs=8)

        def ew_copy(eng, dst, src):
            if eng == "s":
                nc.scalar.copy(out=dst, in_=src)
            else:
                nc.vector.tensor_copy(out=dst, in_=src)

        sw_b = keep.tile([P, 3], BF16, name="sw_b")
        bias_b = [keep.tile([P, 4], BF16, name="bias_b%d" % s) for s in range(2)]
        nc.scalar.dma_start(out=sw_b[:], in_=scoring_weights.partition_broadcast(P))
        nc.scalar.dma_start(out=bias_b[0][:], in_=bk.rearrange("(p t) -> p t", t=4))
        nc.scalar.dma_start(out=bias_b[1][:], in_=bq.rearrange("(p t) -> p t", t=4))

        def w_src(w, h):
            return w.rearrange("(p t) i -> p t i", t=4)[:, 2 * h : 2 * h + 2, :]

        def k_src(b, h):
            return key[b, 256 * h : 256 * h + 256, :].rearrange("(p n) i -> p n i", n=2)

        def q_src(b, h):
            return query[b].rearrange("(p n) i -> p n i", n=4)[:, 2 * h : 2 * h + 2, :]

        srcs = [w_src(Wk, 0), w_src(Wk, 1), k_src(0, 0), k_src(0, 1),
                w_src(Wq, 0), w_src(Wq, 1), q_src(0, 0), q_src(0, 1),
                k_src(1, 0), k_src(1, 1), q_src(1, 0), q_src(1, 1)]
        xs = {}
        for i in [0,2,3,1,4,6,7,5,8,9,10,11]:
            x = keep.tile([P, 1024], BF16, name="xs%d" % i)
            nc.sync.dma_start(out=x[:].rearrange("p (n i) -> p n i", n=2), in_=srcs[i])
            xs[i] = x

        ident = keep.tile([P, P], F32, name="ident")
        make_identity(nc, ident[:])
        mhalf = keep.tile([P, 4], F32, name="mhalf")
        nc.gpsimd.memset(mhalf[:], -0.5)
        tiny = keep.tile([P, 1], F32, name="tiny")
        nc.gpsimd.memset(tiny[:], 1e-15)

        bias_f = [keep.tile([P, 4], F32, name="bias_f%d" % s) for s in range(2)]
        wf = keep.tile([P, 3], F32, name="wf")
        wmax = keep.tile([P, 1], F32, name="wmax")
        wd = keep.tile([P, 3], F32, name="wd")
        nc.gpsimd.tensor_copy(out=wf[:], in_=sw_b[:])
        nc.gpsimd.tensor_scalar(out=wmax[:], in0=wf[:, 0:1], scalar1=wf[:, 1:2], scalar2=wf[:, 2:3],
                                op0=ALU.max, op1=ALU.max)
        nc.gpsimd.tensor_scalar(out=wd[:], in0=wf[:], scalar1=wmax[:, 0:1], scalar2=0.0,
                                op0=ALU.subtract, op1=ALU.add)
        nc.gpsimd.tensor_copy(out=bias_f[0][:], in_=bias_b[0][:])
        nc.gpsimd.tensor_copy(out=bias_f[1][:], in_=bias_b[1][:])

        we = keep.tile([P, 3], F32, name="we")
        wsum = keep.tile([P, 1], F32, name="wsum")
        rws = keep.tile([P, 1], F32, name="rws")
        cst = keep.tile([P, 8], F32, name="cst")
        W0, W1, W2, W2SQ, CC = 0, 1, 2, 3, 4

        def col(c):
            return cst[:, c : c + 1]

        def EXPW():
            nc.scalar.activation(out=we[:], in_=wd[:], func=ACT.Exp, accum_out=wsum[:])

        def WC(step):
            v = nc.vector
            if step == 0:
                v.reciprocal(out=rws[:], in_=wsum[:])
            elif step == 1:
                v.tensor_scalar(out=cst[:, 0:3], in0=we[:], scalar1=rws[:, 0:1], scalar2=None, op0=ALU.mult)
            elif step == 2:
                v.tensor_tensor(out=col(W2SQ), in0=col(W2), in1=col(W2), op=ALU.mult)
            else:
                v.tensor_scalar(out=col(CC), in0=col(W1), scalar1=1e8, scalar2=col(W0), op0=ALU.mult, op1=ALU.add)

        in_c = [keep.tile([P, 512], U32, name="in_c%d" % o, align_bytes=64) for o in range(6)]
        in_s = [keep.tile([P, 512], U8, name="in_s%d" % o, align_bytes=64) for o in range(6)]
        xt = {}
        grp = {}

        def T(i):
            t = bank("xt%d" % i, "tp")
            xw = xs[i][:].bitcast(F32)
            for nn in range(2):
                for u in range(2):
                    nc.tensor.transpose(t[:, u * 256 + nn * 128 : u * 256 + nn * 128 + 128],
                                        xw[:, nn * 256 + u * 128 : nn * 256 + u * 128 + 128], ident[:])
            xt[i] = t

        def EV(i, eng):
            o, h = i // 2, i % 2
            if o not in grp:
                grp[o] = keep.tile([P, 2048], BF16, name="grp%d" % o, align_bytes=64)
            words = grp[o][:, 1024 * h : 1024 * h + 1024].bitcast(F32)
            if o in (1, 4):
                ew_copy(eng, words.rearrange("p (r n u) -> p r n u", n=2, u=2),
                        xt[i][:].rearrange("p (u n r) -> p r n u", n=2, u=2))
            else:
                ew_copy(eng, words.rearrange("p (r u) -> p r u", u=2), xt[i][:].rearrange("p (u r) -> p r u", u=2))

        def QH(i):
            o, h = i // 2, i % 2
            nc.vector.quantize_mx(out=in_c[o][:, 256 * h : 256 * h + 256].bitcast(FP8X4),
                                  scales=in_s[o][:, 256 * h : 256 * h + 256],
                                  in_=grp[o][:, 1024 * h : 1024 * h + 1024])

        def QZ(o):
            nc.vector.quantize_mx(out=in_c[o][:].bitcast(FP8X4), scales=in_s[o][:], in_=grp[o][:])

        g_w = [0, 2, 0, 2]
        g_x = [1, 3, 4, 5]
        pj = {}
        ft = {}
        gq = {}
        qk_c = [keep.tile([P, 512], U32, name="qk_c%d" % g, align_bytes=64) for g in range(4)]
        qk_s = [keep.tile([P, 512], U8, name="qk_s%d" % g, align_bytes=64) for g in range(4)]

        def PJ(g, t):
            a = bank("pj%d_%d" % (g, t), "pj")
            nc.tensor.matmul_mx(out=a[:],
                                lhsT=in_c[g_w[g]][:, t * 128 : t * 128 + 128].bitcast(FP8X4),
                                lhsT_scale=in_s[g_w[g]][:, t * 128 : t * 128 + 128],
                                rhs=in_c[g_x[g]][:].bitcast(FP8X4), rhs_scale=in_s[g_x[g]][:],
                                start=True, stop=True)
            pj[(g, t)] = a

        def TH(g, t):
            if g not in ft:
                ft[g] = work.tile([P, 2048], F32, name="f%d" % g, tag="f", bufs=BUFS["f"])
            nc.scalar.activation(out=ft[g][:, t * 512 : t * 512 + 512], in_=pj[(g, t)][:], func=ACT.Tanh,
                                 bias=bias_f[g % 2][:, t : t + 1], scale=1.0)

        def RG(g):
            r = work.tile([P, 2048], BF16, name="gq%d" % g, tag="gq", bufs=BUFS["gq"], align_bytes=64)
            nc.vector.tensor_copy(out=r[:].rearrange("p (c i t) -> p c t i", i=4, t=4),
                                  in_=ft[g][:].rearrange("p (t c i) -> p c t i", i=4, t=4))
            gq[g] = r

        def QG(g):
            nc.vector.quantize_mx(out=qk_c[g][:].bitcast(FP8X4), scales=qk_s[g][:], in_=gq[g][:])

        tq = {}
        n2 = [keep.tile([P, 4], F32, name="n2_%d" % g) for g in range(4)]
        rn = [keep.tile([P, 4], F32, name="rn%d" % g) for g in range(4)]

        def TQ(g, n):
            a = bank("tq%d_%d" % (g, n), "tq")
            for t in range(4):
                nc.tensor.transpose(a[:, t * 128 : t * 128 + 128],
                                    ft[g][:, t * 512 + n * 128 : t * 512 + n * 128 + 128], ident[:])
            tq[(g, n)] = a

        def SQ(g, n):
            j = work.tile([P, 512], BF16, name="jk%d_%d" % (g, n), tag="junk", bufs=BUFS["junk"])
            nc.scalar.activation(out=j[:], in_=tq[(g, n)][:], func=ACT.Square, bias=tiny[:, 0:1],
                                 accum_out=n2[g][:, n : n + 1])

        def KD(g, n):
            a = bank("kd%d_%d" % (g, n), "tq")
            for t in range(4):
                x = ft[g][:, t * 512 + n * 128 : t * 512 + n * 128 + 128]
                nc.tensor.matmul(a[:, 0:128], lhsT=x, rhs=x, start=(t == 0), stop=(t == 3))
            tq[(g, n)] = a

        def KE(g, n):
            j = work.tile([P, P], F32, name="kj%d_%d" % (g, n), tag="kj", bufs=2)
            nc.vector.scalar_tensor_tensor(out=j[:], in0=tq[(g, n)][:, 0:128], scalar=TINY, in1=ident[:],
                                           op0=ALU.max, op1=ALU.mult, accum_out=n2[g][:, n : n + 1])

        def PW(g, n0=0, c=4):
            nc.gpsimd.tensor_tensor(out=rn[g][:, n0 : n0 + c], in0=n2[g][:, n0 : n0 + c], in1=mhalf[:, 0:c],
                                    op=ALU.pow)

        qn = [keep.tile([P, 4], F32, name="qn%d" % g) for g in range(4)]

        def SR(g):
            nc.scalar.activation(out=qn[g][:], in_=n2[g][:], func=ACT.Sqrt)

        def RV(g):
            nc.vector.reciprocal(out=rn[g][:], in_=qn[g][:])

        kn2_sb = [keep.tile([P, 512], F32, name="kn2_sb%d" % b) for b in range(2)]
        rkb_sb = [keep.tile([P, 512], F32, name="rkb_sb%d" % b) for b in range(2)]
        bc = {}

        def spread(name, v):
            a = bank(name, "tq")
            for n in range(4):
                nc.tensor.transpose(a[:, n * 128 : n * 128 + 128], v[:, n : n + 1].to_broadcast([P, P]), ident[:])
            return a

        def BK(b):
            bc[("k", b)] = spread("bck%d" % b, n2[2 * b])

        def BR(b):
            bc[("r", b)] = spread("bcr%d" % b, rn[2 * b])

        def CK(b, eng):
            ew_copy(eng, kn2_sb[b][:], bc[("k", b)][:])

        def CR(b, eng):
            nc.scalar.activation(out=rkb_sb[b][:], in_=bc[("r", b)][:], func=ACT.Copy, scale=col(W1))

        dot = {}
        gp = {}
        zt = [keep.tile([P, 2048], F32, name="zt%d" % b) for b in range(2)]
        t2 = [keep.tile([P, 2048], F32, name="t2_%d" % b) for b in range(2)]
        mn = [keep.tile([P, 4], F32, name="mn%d" % b) for b in range(2)]
        ssum = [keep.tile([P, 4], F32, name="ssum%d" % b) for b in range(2)]
        rs = [keep.tile([P, 4], F32, name="rs%d" % b) for b in range(2)]

        def sl(t, n0, c=1):
            return t[:, 512 * n0 : 512 * (n0 + c)]

        def D(b, n):
            a = bank("dot%d_%d" % (b, n), "dt")
            nc.tensor.matmul_mx(out=a[:],
                                lhsT=qk_c[2 * b + 1][:, n * 128 : n * 128 + 128].bitcast(FP8X4),
                                lhsT_scale=qk_s[2 * b + 1][:, n * 128 : n * 128 + 128],
                                rhs=qk_c[2 * b][:].bitcast(FP8X4), rhs_scale=qk_s[2 * b][:],
                                start=True, stop=True)
            dot[(b, n)] = a

        def A(b, n):
            nc.vector.scalar_tensor_tensor(out=sl(zt[b], n), in0=dot[(b, n)][:], scalar=-2.0, in1=kn2_sb[b][:],
                                           op0=ALU.mult, op1=ALU.add)

        def B(b, n):
            nc.vector.tensor_scalar(out=sl(zt[b], n), in0=sl(zt[b], n), scalar1=n2[2 * b + 1][:, n : n + 1],
                                    scalar2=0.0, op0=ALU.add, op1=ALU.max)

        def C(b, n0, c):
            nc.scalar.activation(out=sl(zt[b], n0, c), in_=sl(zt[b], n0, c), func=ACT.Sqrt, scale=col(W2SQ))

        def DG(b, n, eng="g"):
            g = work.tile([P, 512], F32, name="gp%d_%d" % (b, n), tag="gp", bufs=BUFS["gp"])
            if eng == "g":
                nc.gpsimd.tensor_scalar(out=g[:], in0=rkb_sb[b][:], scalar1=rn[2 * b + 1][:, n : n + 1], scalar2=col(W0),
                                        op0=ALU.mult, op1=ALU.add)
            elif eng == "v":
                nc.vector.tensor_scalar(out=g[:], in0=rkb_sb[b][:], scalar1=rn[2 * b + 1][:, n : n + 1], scalar2=col(W0),
                                        op0=ALU.mult, op1=ALU.add)
            else:
                nc.scalar.activation(out=g[:], in_=rkb_sb[b][:], func=ACT.Identity, bias=col(W0),
                                     scale=rn[2 * b + 1][:, n : n + 1])
            gp[(b, n)] = g

        def E(b, n):
            nc.vector.scalar_tensor_tensor(out=sl(t2[b], n), in0=gp[(b, n)][:], scalar=col(CC), in1=dot[(b, n)][:],
                                           op0=ALU.min, op1=ALU.mult)

        def F(b, n0, c, eng="v"):
            e = nc.gpsimd if eng == "g" else nc.vector
            e.tensor_tensor(out=sl(t2[b], n0, c), in0=sl(zt[b], n0, c), in1=sl(t2[b], n0, c), op=ALU.subtract)

        def M(b, n0, c):
            nc.vector.tensor_reduce(out=mn[b][:, n0 : n0 + c], in_=sl(t2[b], n0, c).rearrange("p (n j) -> p n j", n=c),
                                    axis=AX.X, op=ALU.min)

        def H(b, n):
            nc.scalar.activation(out=sl(t2[b], n), in_=sl(t2[b], n), func=ACT.Exp, bias=mn[b][:, n : n + 1], scale=-1.0,
                                 accum_out=ssum[b][:, n : n + 1])

        def R(b, n0, c):
            nc.vector.reciprocal(out=rs[b][:, n0 : n0 + c], in_=ssum[b][:, n0 : n0 + c])

        def I(b, n, eng):
            t = sl(t2[b], n)
            r = rs[b][:, n : n + 1]
            if eng == "s":
                nc.scalar.activation(out=t, in_=t, func=ACT.Copy, scale=r)
            elif eng == "g":
                nc.gpsimd.tensor_scalar(out=t, in0=t, scalar1=r, scalar2=0.0, op0=ALU.mult, op1=ALU.add)
            else:
                nc.vector.tensor_scalar(out=t, in0=t, scalar1=r, scalar2=None, op0=ALU.mult)

        def ST(b, n0, c):
            nc.sync.dma_start(out=out[b].rearrange("(r n) j -> r n j", n=4)[:, n0 : n0 + c, :],
                              in_=sl(t2[b], n0, c).rearrange("p (n j) -> p n j", n=c))


        IN0 = (0, 2, 3, 1, 4, 6, 7, 5)
        for k, i in enumerate(IN0):
            T(i)
            EV(i, "v" if k in (1, 5) else "s")
            if k == 0:
                EXPW()
            if k:
                QH(IN0[k - 1])
            if k > 3:
                WC(k - 4)
        for t in range(2):
            PJ(0, t)
        QH(5)
        for t in range(2, 4):
            PJ(0, t)
        T(8); T(9); T(10); T(11)
        EV(8, "v"); EV(9, "v"); QH(8); QH(9)
        for t in range(4):
            TH(0, t)
        for t in range(4):
            PJ(1, t)
        EV(11, "s")
        RG(0)
        EV(10, "v"); QG(0)
        QH(10); QH(11)
        KD(0, 0)
        for t in range(4):
            TH(1, t)
        for t in range(4):
            PJ(2, t)
        KD(0, 1)
        KE(0, 0)
        for t in range(4):
            TH(2, t)
        for t in range(4):
            PJ(3, t)
        KD(0, 2)
        RG(1); KE(0, 1); QG(1)
        TQ(0, 3)
        for t in range(4):
            TH(3, t)
        SQ(0, 3)
        for n in range(4):
            TQ(1, n)
        RG(2); KE(0, 2)
        PW(0); BK(0)
        for n in range(4):
            D(0, n)
        SQ(1, 0); CK(0, "s"); SQ(1, 1)
        PW(1, 0, 2)
        BR(0)
        SQ(1, 2); SQ(1, 3); CR(0, "s")
        QG(2)
        RG(3)
        QG(3)
        for n in range(4):
            A(0, n)
        PW(1, 2, 2)
        for n in range(4):
            KD(2, n)
        for n in range(4):
            B(0, n)
        for n in range(4):
            C(0, n, 1)
        DG(0, 2, "g"); DG(0, 3, "g")
        KE(2, 0); KE(2, 1)
        DG(0, 0, "v"); DG(0, 1, "v")
        TQ(3, 0); TQ(3, 1)
        E(0, 0); KE(2, 2); E(0, 1); KE(2, 3); E(0, 2); E(0, 3)
        BK(1); CK(1, "s")
        for n in range(4):
            D(1, n)
        TQ(3, 2); TQ(3, 3)
        SR(2)
        for n in range(4):
            SQ(3, n)
        SR(3)
        for n in range(3):
            F(0, n, 1, "g")
        F(0, 3, 1)
        A(1, 0); RV(2); A(1, 1); A(1, 2); A(1, 3)
        BR(1); CR(1, "s")
        for n in range(4):
            B(1, n); C(1, n, 1)
        RV(3)
        for n in (0, 1, 2, 3):
            DG(1, n, "g")
        for n in range(4):
            M(0, n, 1)
        for n in range(4):
            H(0, n)
        for n in range(4):
            E(1, n)
        F(1, 0, 1, "g"); F(1, 1, 1, "g")
        F(1, 2, 1)
        R(0, 0, 2)
        F(1, 3, 1)
        I(0, 0, "s"); ST(0, 0, 1)
        M(1, 2, 1); H(1, 2)
        I(0, 1, "v"); ST(0, 1, 1)
        M(1, 3, 1); H(1, 3)
        R(0, 2, 2)
        M(1, 0, 1); H(1, 0)
        I(0, 2, "v"); ST(0, 2, 1)
        M(1, 1, 1); H(1, 1)
        I(0, 3, "v"); ST(0, 3, 1)
        R(1, 2, 2)
        I(1, 2, "v"); ST(1, 2, 1)
        I(1, 3, "v"); ST(1, 3, 1)
        for n in (0, 1):
            R(1, n, 1)
        for n in (0, 1):
            I(1, n, "v"); ST(1, n, 1)
